import numpy as np
import ml_dtypes


def mxq(x, axis, fmt="e4m3"):
    dtype, down = {"e4m3": (ml_dtypes.float8_e4m3fn, 7), "e5m2": (ml_dtypes.float8_e5m2, 14)}[fmt]
    v = np.moveaxis(np.asarray(x, np.float32).astype(ml_dtypes.bfloat16).astype(np.float64), axis, -1)
    blocks = v.reshape(v.shape[:-1] + (-1, 32))
    amax = np.abs(blocks).max(-1, keepdims=True)
    byte = np.maximum(np.where(amax > 0, np.frexp(amax)[1] - 1 + 127, 0) - down, 1)
    scale = np.exp2(byte - 127.0)
    codes = (blocks / scale).astype(np.float32).astype(dtype).astype(np.float64)
    return np.moveaxis((codes * scale).reshape(v.shape), -1, axis)


WIDE = False


def mx_kscale(k):
    if not WIDE:
        return np.ones(k)
    levels = np.array([10, -10, 5, -5, 0])
    if k % 512:
        return np.exp2(np.random.permutation(np.resize(levels, k // 32))).repeat(32)
    a = np.empty((k // 512, 16))
    for p in range(k // 512):
        a[p, :8] = np.random.permutation(np.resize(levels, 8))
        for g in range(8):
            far = levels[np.abs(levels - a[p, g]) >= 10]
            a[p, g + 8] = far[np.random.randint(len(far))]
    return np.exp2(a.ravel()).repeat(32)


BF16 = ml_dtypes.bfloat16


def bf(x):
    return np.asarray(x, np.float32).astype(BF16)


def f64(x):
    return np.asarray(x).astype(np.float64)


B, K, N, H, W = 1, 4096, 1024, 32, 32
NUM_ITERS = 5
TEMP = 0.1


def logsumexp(a, axis):
    m = a.max(axis=axis, keepdims=True)
    return m + np.log(np.exp(a - m).sum(axis=axis, keepdims=True))


def setup_inputs():
    s = mx_kscale(H * W).reshape(H, W)
    return {"pred_masks": bf(np.random.standard_normal((B, K, H, W)) * s),
            "gt_masks": bf(np.random.standard_normal((N, H, W)) * 0.5 / np.sqrt(H * W) / s)}


def reference(pred_masks, gt_masks):
    p = f64(pred_masks).reshape(B, K, H * W)
    g = f64(gt_masks).reshape(N, H * W)
    dot = mxq(p, 2, "e4m3") @ mxq(g, 1, "e4m3").T
    cost = 1.0 - dot
    log_alpha = -cost / TEMP
    for _ in range(NUM_ITERS):
        log_alpha = log_alpha - logsumexp(log_alpha, 2)
        log_alpha = log_alpha - logsumexp(log_alpha, 1)
    return np.exp(log_alpha)

@@ -1,0 +1,454 @@
+from contextlib import ExitStack
+
+import concourse.mybir as mybir
+from concourse.masks import make_identity
+
+F32 = mybir.dt.float32
+BF16 = mybir.dt.bfloat16
+U32 = mybir.dt.uint32
+U8 = mybir.dt.uint8
+FP8X4 = mybir.dt.float8_e4m3fn_x4
+ALU = mybir.AluOpType
+ACT = mybir.ActivationFunctionType
+AX = mybir.AxisListType
+
+P = 128
+ROWS = 4096
+COLS = 1024
+CONTR = 1024
+RT = ROWS // P
+CC = COLS // P
+NP = 22
+NV = RT - NP
+NCOL = 2
+ITERS = 5
+INV_TEMP = 10.0
+KB = 1024
+EARLY = 2
+GPAIRS = 5
+GT = NP // 2
+REBUILT = 8
+MID = 13
+COL_SLOTS = {26: [0], 27: [1], 28: [2], 29: [3], 30: [4], 31: [5], 32: [6, 7]}
+FLOPS = 2 * ROWS * COLS * CONTR
+
+OFF_EAH = 0
+OFF_EAL = OFF_EAH + NP * 2 * KB
+OFF_EB = OFF_EAL + NP * 2 * KB
+OFF_EV = OFF_EB + NP * 4 * KB
+OFF_MISC = OFF_EV + NV * 4 * KB
+OFF_GRAW = OFF_EAH + (NP - 8) * 2 * KB
+OFF_GGRP = OFF_EAL + (NP - 8) * 2 * KB
+OFF_GC = OFF_MISC
+OFF_GS = OFF_MISC + 8 * KB
+OFF_ACCH = OFF_MISC
+OFF_ACCL = OFF_MISC + 2 * KB
+OFF_JUNK = OFF_MISC + 4 * KB
+OFF_BCS = OFF_MISC + 6 * KB
+OFF_GRP = OFF_MISC + 10 * KB
+OFF_COD = OFF_MISC + 14 * KB
+OFF_PLN = OFF_MISC + 17 * KB
+OFF_ACC = OFF_PLN + 3 * 256
+
+
+def tile_differentiablematcher_t_kernel(tc, pred_masks, gt_masks, out):
+    nc = tc.nc
+    pv = pred_masks.rearrange("b (p t) h w -> (b p) t (h w)", t=RT)
+    gv = gt_masks.rearrange("(c p) h w -> p c (h w)", p=P)
+    ov = out.rearrange("b (p t) n -> (b p) t n", t=RT)
+
+    with ExitStack() as ctx:
+        big = ctx.enter_context(tc.tile_pool(name="big", bufs=1))
+        small = ctx.enter_context(tc.tile_pool(name="small", bufs=1))
+        tiny = ctx.enter_context(tc.tile_pool(name="tiny", bufs=4))
+        ps = ctx.enter_context(tc.psum_pool(name="ps", bufs=1))
+        ctx.enter_context(tc.manual_schedule())
+
+        def bank(b, shape, dtype, name):
+            return ps.tile(shape, dtype, name=name, tag="bk%d" % b)
+
+        g_raw = big.tile([P, CC, CONTR], BF16, name="g_raw", offset=OFF_GRAW)
+        for q in range(4):
+            nc.sync.dma_start(out=g_raw[:, 2 * q:2 * q + 2, :], in_=gv[:, 2 * q:2 * q + 2, :])
+        p_raw = []
+        for n in range(RT // 2):
+            if 2 * n < NP:
+                off = OFF_EB + 2 * n * 4 * KB
+            else:
+                off = OFF_EV + (2 * n - NP + 1) * 4 * KB
+            r = big.tile([P, 2, CONTR], BF16, name="p_raw%d" % n, offset=off)
+            nc.sync.dma_start(out=r[:], in_=pv[:, 2 * n:2 * n + 2, :])
+            p_raw.append(r)
+
+        ident_f = small.tile([P, P], F32, name="ident_f")
+        make_identity(nc, ident_f[:])
+        ident_b = small.tile([P, P], BF16, name="ident_b")
+        make_identity(nc, ident_b[:])
+        onescol = small.tile([P, NCOL], BF16, name="onescol")
+        nc.vector.memset(onescol[:], 0.0)
+        nc.vector.memset(onescol[:, 0:1], 1.0)
+        mva = small.tile([P, NP, NCOL], BF16, name="mva")
+        nc.vector.memset(mva[:], 0.0)
+        mvb = small.tile([P, CC, NCOL], BF16, name="mvb")
+        nc.vector.memset(mvb[:], 0.0)
+        rs = small.tile([P, RT, 2], F32, name="rs")
+        s_all = small.tile([P, RT], F32, name="s_all")
+        a_all = small.tile([P, RT], F32, name="a_all")
+        svh = small.tile([P, NV, 2], F32, name="svh")
+        tt = small.tile([P, CC], F32, name="tt")
+        bv = small.tile([P, CC], F32, name="bv")
+
+        g_grp = big.tile([P, 2, 4 * COLS], BF16, name="g_grp", offset=OFF_GGRP, align_bytes=64)
+        g_grp_w = g_grp[:].bitcast(F32).rearrange("p g (j u) -> p g j u", u=2)
+        gc = big.tile([P, 2, COLS], U32, name="gc", offset=OFF_GC, align_bytes=64)
+        gs = big.tile([P, 2, COLS], U8, name="gs", offset=OFF_GS, align_bytes=64)
+        for half in range(2):
+            for jc in range(4 * half, 4 * half + 4):
+                tpg = bank(jc, [P, 2, 2, P], F32, "tpg")
+                src = g_raw[:, jc, :].bitcast(F32)
+                for g in range(2):
+                    for u in range(2):
+                        lo = 256 * g + u
+                        nc.tensor.transpose(tpg[:, g, u, :], src[:, lo:lo + 255:2], ident_f[:])
+                dst = g_grp_w[:, :, jc * P:(jc + 1) * P, :]
+                if jc % 2 == 0:
+                    nc.vector.tensor_copy(out=dst, in_=tpg[:].rearrange("p g u w -> p g w u"))
+                else:
+                    nc.scalar.copy(out=dst, in_=tpg[:].rearrange("p g u w -> p g w u"))
+            for g in range(2):
+                nc.vector.quantize_mx(
+                    out=gc[:, g, half * 512:(half + 1) * 512].bitcast(FP8X4),
+                    scales=gs[:, g, half * 512:(half + 1) * 512],
+                    in_=g_grp[:, g, half * 2048:(half + 1) * 2048],
+                )
+
+        grp_of = {}
+        cod_of = {}
+        d_of = {}
+        nb_of = {}
+        e32_of = {}
+        eah = {}
+        eal = {}
+        ebp_of = {}
+        ebh = {}
+        ebl = {}
+        ev = {}
+
+        tp_of = {}
+
+        def do_transposes(t, g):
+            src = p_raw[t // 2][:, t % 2, :].bitcast(F32)
+            if g == 0:
+                tp_of[t] = bank(t % 2, [P, 2, 2, P], F32, "tp")
+            for u in range(2):
+                lo = 256 * g + u
+                nc.tensor.transpose(tp_of[t][:, g, u, :], src[:, lo:lo + 255:2], ident_f[:])
+
+        def do_regroup(t, on_vector):
+            grp = big.tile([P, 4 * 256], BF16, name="grp%d" % (t % 2),
+                           offset=OFF_GRP + (t % 2) * 2 * KB, align_bytes=64)
+            dst = grp[:].bitcast(F32).rearrange("p (g i u) -> p g i u", g=2, u=2)
+            words = tp_of[t][:].rearrange("p g u i -> p g i u")
+            if on_vector:
+                nc.vector.tensor_copy(out=dst, in_=words)
+            else:
+                nc.scalar.copy(out=dst, in_=words)
+            grp_of[t] = grp
+
+        def do_quantise(t):
+            cod = big.tile([P, 256], U32, name="cod%d" % (t % 3),
+                           offset=OFF_COD + (t % 3) * KB, align_bytes=64)
+            pln = big.tile([P, 256], U8, name="pln%d" % (t % 3),
+                           offset=OFF_PLN + (t % 3) * 256, align_bytes=64)
+            nc.vector.quantize_mx(out=cod[:].bitcast(FP8X4), scales=pln[:], in_=grp_of[t][:])
+            cod_of[t] = (cod, pln)
+
+        def do_mx(t, h):
+            cod, pln = cod_of[t]
+            d = bank(2 + 2 * (t % 2) + h, [P, 512], F32, "d")
+            for g in range(2):
+                nc.tensor.matmul_mx(
+                    out=d[:],
+                    lhsT=cod[:, g * P:(g + 1) * P].bitcast(FP8X4),
+                    lhsT_scale=pln[:, g * P:(g + 1) * P],
+                    rhs=gc[:, g, h * 512:(h + 1) * 512].bitcast(FP8X4),
+                    rhs_scale=gs[:, g, h * 512:(h + 1) * 512],
+                    start=(g == 0),
+                    stop=(g == 1),
+                )
+            d_of[(t, h)] = d
+
+        m2_of = {}
+
+        def do_max(t, h):
+            if h == 0:
+                m2_of[t] = tiny.tile([P, 2], F32, name="m2")
+            m2 = m2_of[t]
+            nc.vector.tensor_reduce(out=m2[:, h:h + 1], in_=d_of[(t, h)][:], axis=AX.X, op=ALU.max)
+            if h == 1:
+                nb = tiny.tile([P, 1], F32, name="nb")
+                nc.vector.tensor_scalar(out=nb[:], in0=m2[:, 0:1], scalar1=m2[:, 1:2],
+                                        scalar2=-INV_TEMP, op0=ALU.max, op1=ALU.mult)
+                nb_of[t] = nb
+
+        def do_exp(t):
+            ds = [d_of[(t, 0)], d_of[(t, 1)]]
+            if t < NP:
+                dest = big.tile([P, COLS], F32, name="e32_%d" % (t % 3),
+                                offset=OFF_EV + (4 + 2 * (t % 3)) * 4 * KB)
+                e32_of[t] = dest
+            else:
+                dest = big.tile([P, COLS], F32, name="ev%d" % (t - NP),
+                                offset=OFF_EV + (t - NP) * 4 * KB)
+                ev[t - NP] = dest
+            if t < NP:
+                eah[t] = big.tile([P, COLS], BF16, name="eah%d" % t, offset=OFF_EAH + t * 2 * KB)
+            for h in range(2):
+                hs = slice(h * 512, (h + 1) * 512)
+                nc.scalar.activation(out=dest[:, hs], in_=ds[h][:], func=ACT.Exp,
+                                     bias=nb_of[t][:, 0:1], scale=INV_TEMP,
+                                     accum_out=rs[:, t, h:h + 1])
+                if t < NP:
+                    nc.scalar.activation(out=eah[t][:, hs], in_=ds[h][:], func=ACT.Exp,
+                                         bias=nb_of[t][:, 0:1], scale=INV_TEMP)
+            if t < NP - REBUILT:
+                nc.sync.dma_start(out=ov[:, t, :], in_=dest[:])
+
+        def do_sub(t):
+            lo = big.tile([P, COLS], BF16, name="eal%d" % t, offset=OFF_EAL + t * 2 * KB)
+            for h in range(2):
+                hs = slice(h * 512, (h + 1) * 512)
+                nc.gpsimd.tensor_tensor(out=lo[:, hs], in0=e32_of[t][:, hs], in1=eah[t][:, hs],
+                                        op=ALU.subtract)
+            eal[t] = lo
+
+        def do_eb_transposes(t, part):
+            src = eah[t] if part == 0 else eal[t]
+            ebp = bank(6 + part, [P, CC, P], BF16, "ebp")
+            for jc in range(CC):
+                nc.tensor.transpose(ebp[:, jc, :], src[:, jc * P:(jc + 1) * P], ident_b[:])
+            ebp_of[(t, part)] = ebp
+
+        def do_eb_copy(t, lo_on_vector):
+            for part in range(2):
+                eb = big.tile([P, CC, P], BF16, name="eb%d_%d" % (part, t),
+                              offset=OFF_EB + t * 4 * KB + part * 2 * KB)
+                if part == 1 and lo_on_vector:
+                    nc.vector.tensor_copy(out=eb[:], in_=ebp_of[(t, part)][:])
+                else:
+                    nc.scalar.copy(out=eb[:], in_=ebp_of[(t, part)][:])
+                if part == 0:
+                    ebh[t] = eb
+                else:
+                    ebl[t] = eb
+
+        acc = big.tile([P, COLS], F32, name="acc", offset=OFF_ACC)
+        csp_of = {}
+
+        def split(mv, vec):
+            nc.vector.tensor_copy(out=mv[:, :, 0:1], in_=vec.unsqueeze(2))
+            nc.vector.tensor_tensor(out=mv[:, :, 1:2], in0=vec.unsqueeze(2), in1=mv[:, :, 0:1],
+                                    op=ALU.subtract)
+
+        def a_of_p_tiles(lo, hi, sums):
+            nc.vector.tensor_reduce(out=s_all[:, lo:hi], in_=sums, axis=AX.X, op=ALU.add)
+            nc.vector.reciprocal(out=a_all[:, lo:hi], in_=s_all[:, lo:hi])
+            split(mva[:, lo:hi, :], a_all[:, lo:hi])
+
+        def acc_step(v, h):
+            hs = slice(h * 512, (h + 1) * 512)
+            if v == 0:
+                nc.vector.tensor_scalar(out=acc[:, hs], in0=ev[v][:, hs],
+                                        scalar1=a_all[:, NP:NP + 1], scalar2=None, op0=ALU.mult)
+            else:
+                nc.vector.scalar_tensor_tensor(
+                    out=acc[:, hs], in0=ev[v][:, hs], scalar=a_all[:, NP + v:NP + v + 1],
+                    in1=acc[:, hs], op0=ALU.mult, op1=ALU.add)
+
+        def col_open():
+            csp_of[0] = bank(6, [P, CC, 3, NCOL], F32, "csp")
+
+        def col_pe(jc, g):
+            k = 0
+            for t in range(g * GT, (g + 1) * GT):
+                for ea in (eah[t], eal[t]):
+                    nc.tensor.matmul(csp_of[0][:, jc, g, :], lhsT=ea[:, jc * P:(jc + 1) * P],
+                                     rhs=mva[:, t, :], start=(k == 0), stop=(k == 2 * GT - 1))
+                    k += 1
+
+        for s in range(-3, RT + 2):
+            scalar_full = s <= NP
+            if 0 <= s + 2 < RT:
+                do_regroup(s + 2, scalar_full)
+            if s == NP + 1:
+                a_of_p_tiles(0, NP, rs[:, 0:NP, :])
+            if 0 <= s - 1 < RT:
+                do_exp(s - 1)
+            if 0 <= s - 2 < NP:
+                do_sub(s - 2)
+            if NP <= s - 2 < RT:
+                t = s - 2
+                nc.vector.tensor_reduce(out=s_all[:, t:t + 1], in_=rs[:, t, :], axis=AX.X, op=ALU.add)
+                nc.vector.reciprocal(out=a_all[:, t:t + 1], in_=s_all[:, t:t + 1])
+                acc_step(t - NP, 0)
+                acc_step(t - NP, 1)
+            for h in range(2):
+                if 0 <= s < RT:
+                    do_mx(s, h)
+            for h in range(2):
+                if 0 <= s - 4 < NP:
+                    do_eb_transposes(s - 4, h)
+            for h in range(2):
+                if 0 <= s + 3 < RT:
+                    do_transposes(s + 3, h)
+            for h in range(2):
+                if 0 <= s < RT:
+                    do_max(s, h)
+            if 0 <= s + 2 < RT:
+                do_quantise(s + 2)
+            if 0 <= s - 4 < NP:
+                do_eb_copy(s - 4, scalar_full)
+            for jc in COL_SLOTS.get(s, []):
+                if jc == 0:
+                    col_open()
+                col_pe(jc, 0)
+                col_pe(jc, 1)
+
+        acch = big.tile([P, COLS], BF16, name="acch", offset=OFF_ACCH)
+        accl = big.tile([P, COLS], BF16, name="accl", offset=OFF_ACCL)
+        junk = big.tile([P, 512], F32, name="junk", offset=OFF_JUNK)
+
+        def broadcast_bv():
+            bc = []
+            for h in range(2):
+                b = bank(2 + h, [P, 512], F32, "bc")
+                bc.append(b)
+            for jc in range(CC):
+                o = bc[jc // 4][:, (jc % 4) * P:(jc % 4 + 1) * P]
+                nc.tensor.transpose(o, bv[:, jc:jc + 1].to_broadcast([P, P]), ident_f[:])
+            return bc
+
+        def col_finish(first_left):
+            csp = csp_of[0]
+            for i in range(first_left, 2 * NV):
+                acc_step(i // 2, i % 2)
+                if i >= 2 * NV - 2:
+                    hs = slice((i % 2) * 512, (i % 2 + 1) * 512)
+                    nc.scalar.copy(out=acch[:, hs], in_=acc[:, hs])
+            if first_left >= 2 * NV:
+                for h in range(2):
+                    nc.scalar.copy(out=acch[:, h * 512:(h + 1) * 512], in_=acc[:, h * 512:(h + 1) * 512])
+            for h in range(2):
+                hs = slice(h * 512, (h + 1) * 512)
+                nc.vector.tensor_tensor(out=accl[:, hs], in0=acc[:, hs], in1=acch[:, hs],
+                                        op=ALU.subtract)
+                for jc in range(4 * h, 4 * h + 4):
+                    nc.tensor.matmul(csp[:, jc, 2, :], lhsT=acch[:, jc * P:(jc + 1) * P],
+                                     rhs=onescol[:], start=True, stop=False)
+                    nc.tensor.matmul(csp[:, jc, 2, :], lhsT=accl[:, jc * P:(jc + 1) * P],
+                                     rhs=onescol[:], start=False, stop=True)
+            nc.vector.tensor_reduce(out=tt[:], in_=csp[:], axis=AX.XY, op=ALU.add)
+            nc.vector.reciprocal(out=bv[:], in_=tt[:])
+            split(mvb, bv[:])
+
+        def row_phase():
+            bc = broadcast_bv()
+            rsp = [bank(4 + g, [P, GT, NCOL], F32, "rsp") for g in range(2)]
+            for t in range(NP):
+                k = 0
+                for jc in range(CC):
+                    for eb in (ebh[t], ebl[t]):
+                        nc.tensor.matmul(rsp[t // GT][:, t % GT, :], lhsT=eb[:, jc, :],
+                                         rhs=mvb[:, jc, :],
+                                         start=(k == 0), stop=(k == 2 * CC - 1))
+                        k += 1
+            for i in range(2 * NV):
+                v = i // 2
+                h = i % 2
+                nc.vector.scalar_tensor_tensor(
+                    out=junk[:], in0=ev[v][:, h * 512:(h + 1) * 512], scalar=1.0,
+                    in1=bc[h][:], op0=ALU.mult, op1=ALU.mult,
+                    accum_out=svh[:, v, h:h + 1])
+                if i == MID - 1:
+                    a_of_p_tiles(0, GT, rsp[0][:])
+            nc.vector.tensor_reduce(out=s_all[:, NP:RT], in_=svh[:], axis=AX.X, op=ALU.add)
+            nc.vector.reciprocal(out=a_all[:, NP:RT], in_=s_all[:, NP:RT])
+            for i in range(EARLY):
+                acc_step(i // 2, i % 2)
+            a_of_p_tiles(GT, NP, rsp[1][:])
+
+        def col_phase():
+            col_open()
+            for g in range(2):
+                for jc in range(CC):
+                    col_pe(jc, g)
+            col_finish(EARLY)
+
+        r32 = {}
+        col_finish(2 * NV)
+        for it in range(1, ITERS):
+            row_phase()
+            if it == ITERS - 1:
+                for t in range(0, NP, 2):
+                    r = big.tile([P, 2, COLS], F32, name="r32_%d" % t, offset=OFF_EB + t * 4 * KB)
+                    if t < NP - REBUILT:
+                        nc.sync.dma_start(out=r[:], in_=ov[:, t:t + 2, :])
+                    r32[t] = r
+            col_phase()
+
+        bc = broadcast_bv()
+        bcs = big.tile([P, COLS], F32, name="bcs", offset=OFF_BCS)
+        for h in range(2):
+            nc.scalar.copy(out=bcs[:, h * 512:(h + 1) * 512], in_=bc[h][:])
+        g_pairs = [t for t in range(0, NP, 2) if t < 2 * GPAIRS]
+        v_pairs = [t for t in range(0, NP - REBUILT, 2) if t >= 2 * GPAIRS]
+        r_tiles = list(range(NP - REBUILT, NP))
+        sum_banks = [(0, 1), (4, 5), (6, 7)]
+        sums = {}
+
+        def rebuild(i):
+            t = r_tiles[i]
+            for h in range(2):
+                hs = slice(h * 512, (h + 1) * 512)
+                esum = bank(sum_banks[i % 3][h], [P, 512], F32, "esum")
+                nc.tensor.matmul(esum[:], lhsT=ident_b[:], rhs=eah[t][:, hs], start=True, stop=False)
+                nc.tensor.matmul(esum[:], lhsT=ident_b[:], rhs=eal[t][:, hs], start=False, stop=True)
+                sums[(t, h)] = esum
+
+        for i in range(3):
+            rebuild(i)
+        for t in g_pairs:
+            for e in range(2):
+                nc.scalar.activation(out=r32[t][:, e, :], in_=r32[t][:, e, :], func=ACT.Copy,
+                                     scale=a_all[:, t + e:t + e + 1])
+        for t in g_pairs:
+            for e in range(2):
+                nc.gpsimd.tensor_tensor(out=r32[t][:, e, :], in0=r32[t][:, e, :], in1=bcs[:],
+                                        op=ALU.mult)
+            nc.scalar.dma_start(out=ov[:, t:t + 2, :], in_=r32[t][:])
+        for v in range(NV):
+            for h in range(2):
+                hs = slice(h * 512, (h + 1) * 512)
+                nc.vector.scalar_tensor_tensor(
+                    out=ev[v][:, hs], in0=ev[v][:, hs], scalar=a_all[:, NP + v:NP + v + 1],
+                    in1=bc[h][:], op0=ALU.mult, op1=ALU.mult)
+            nc.sync.dma_start(out=ov[:, NP + v, :], in_=ev[v][:])
+        for i, t in enumerate(r_tiles):
+            for h in range(2):
+                hs = slice(h * 512, (h + 1) * 512)
+                nc.vector.scalar_tensor_tensor(
+                    out=r32[t - t % 2][:, t % 2, hs], in0=sums[(t, h)][:],
+                    scalar=a_all[:, t:t + 1], in1=bcs[:, hs], op0=ALU.mult, op1=ALU.mult)
+            if i + 3 < REBUILT:
+                rebuild(i + 3)
+            if t % 2 == 1:
+                nc.sync.dma_start(out=ov[:, t - 1:t + 1, :], in_=r32[t - 1][:])
+        for t in v_pairs:
+            for e in range(2):
+                for h in range(2):
+                    hs = slice(h * 512, (h + 1) * 512)
+                    nc.vector.scalar_tensor_tensor(
+                        out=r32[t][:, e, hs], in0=r32[t][:, e, hs],
+                        scalar=a_all[:, t + e:t + e + 1], in1=bc[h][:],
+                        op0=ALU.mult, op1=ALU.mult)
+            nc.sync.dma_start(out=ov[:, t:t + 2, :], in_=r32[t][:])

@@ -20,15 +20,16 @@ RT = ROWS // P
 CC = COLS // P
 NP = 22
 NV = RT - NP
-NCOL = 2
+NCOL = 3
 ITERS = 5
 INV_TEMP = 10.0
 KB = 1024
-EARLY = 2
+VR = 6
+TICK = 64
+BURST = (512, 256, 128)
 GPAIRS = 5
 GT = NP // 2
 REBUILT = 8
-MID = 13
 COL_SLOTS = {26: [0], 27: [1], 28: [2], 29: [3], 30: [4], 31: [5], 32: [6, 7]}
 FLOPS = 2 * ROWS * COLS * CONTR
 
@@ -41,10 +42,9 @@ OFF_GRAW = OFF_EAH + (NP - 8) * 2 * KB
 OFF_GGRP = OFF_EAL + (NP - 8) * 2 * KB
 OFF_GC = OFF_MISC
 OFF_GS = OFF_MISC + 8 * KB
-OFF_ACCH = OFF_MISC
-OFF_ACCL = OFF_MISC + 2 * KB
-OFF_JUNK = OFF_MISC + 4 * KB
-OFF_BCS = OFF_MISC + 6 * KB
+OFF_JUNK = OFF_MISC + 2 * KB
+OFF_BCS = OFF_MISC + 4 * KB
+OFF_SJUNK = OFF_MISC + 8 * KB + 512
 OFF_GRP = OFF_MISC + 10 * KB
 OFF_COD = OFF_MISC + 14 * KB
 OFF_PLN = OFF_MISC + 17 * KB
@@ -84,9 +84,6 @@ def tile_differentiablematcher_t_kernel(tc, pred_masks, gt_masks, out):
         make_identity(nc, ident_f[:])
         ident_b = small.tile([P, P], BF16, name="ident_b")
         make_identity(nc, ident_b[:])
-        onescol = small.tile([P, NCOL], BF16, name="onescol")
-        nc.vector.memset(onescol[:], 0.0)
-        nc.vector.memset(onescol[:, 0:1], 1.0)
         mva = small.tile([P, NP, NCOL], BF16, name="mva")
         nc.vector.memset(mva[:], 0.0)
         mvb = small.tile([P, CC, NCOL], BF16, name="mvb")
@@ -95,13 +92,21 @@ def tile_differentiablematcher_t_kernel(tc, pred_masks, gt_masks, out):
         s_all = small.tile([P, RT], F32, name="s_all")
         a_all = small.tile([P, RT], F32, name="a_all")
         svh = small.tile([P, NV, 2], F32, name="svh")
+        acs = small.tile([P, CC], F32, name="acs")
         tt = small.tile([P, CC], F32, name="tt")
         bv = small.tile([P, CC], F32, name="bv")
 
         g_grp = big.tile([P, 2, 4 * COLS], BF16, name="g_grp", offset=OFF_GGRP, align_bytes=64)
         g_grp_w = g_grp[:].bitcast(F32).rearrange("p g (j u) -> p g j u", u=2)
-        gc = big.tile([P, 2, COLS], U32, name="gc", offset=OFF_GC, align_bytes=64)
-        gs = big.tile([P, 2, COLS], U8, name="gs", offset=OFF_GS, align_bytes=64)
+        gc = {}
+        gs = {}
+        for g in range(2):
+            for half in range(2):
+                q = 2 * g + half
+                gc[(g, half)] = big.tile([P, 512], U32, name="gc%d" % q,
+                                         offset=OFF_GC + q * 2 * KB, align_bytes=64)
+                gs[(g, half)] = big.tile([P, 512], U8, name="gs%d" % q,
+                                         offset=OFF_GS + q * 512, align_bytes=64)
         for half in range(2):
             for jc in range(4 * half, 4 * half + 4):
                 tpg = bank(jc, [P, 2, 2, P], F32, "tpg")
@@ -117,8 +122,8 @@ def tile_differentiablematcher_t_kernel(tc, pred_masks, gt_masks, out):
                     nc.scalar.copy(out=dst, in_=tpg[:].rearrange("p g u w -> p g w u"))
             for g in range(2):
                 nc.vector.quantize_mx(
-                    out=gc[:, g, half * 512:(half + 1) * 512].bitcast(FP8X4),
-                    scales=gs[:, g, half * 512:(half + 1) * 512],
+                    out=gc[(g, half)][:].bitcast(FP8X4),
+                    scales=gs[(g, half)][:],
                     in_=g_grp[:, g, half * 2048:(half + 1) * 2048],
                 )
 
@@ -171,8 +176,8 @@ def tile_differentiablematcher_t_kernel(tc, pred_masks, gt_masks, out):
                     out=d[:],
                     lhsT=cod[:, g * P:(g + 1) * P].bitcast(FP8X4),
                     lhsT_scale=pln[:, g * P:(g + 1) * P],
-                    rhs=gc[:, g, h * 512:(h + 1) * 512].bitcast(FP8X4),
-                    rhs_scale=gs[:, g, h * 512:(h + 1) * 512],
+                    rhs=gc[(g, h)][:].bitcast(FP8X4),
+                    rhs_scale=gs[(g, h)][:],
                     start=(g == 0),
                     stop=(g == 1),
                 )
@@ -245,15 +250,19 @@ def tile_differentiablematcher_t_kernel(tc, pred_masks, gt_masks, out):
         acc = big.tile([P, COLS], F32, name="acc", offset=OFF_ACC)
         csp_of = {}
 
-        def split(mv, vec):
-            nc.vector.tensor_copy(out=mv[:, :, 0:1], in_=vec.unsqueeze(2))
+        def inverse_and_halves(vec, mv, sums):
+            nc.vector.reciprocal(out=vec, in_=sums)
+            with nc.allow_low_precision(reason="the high half; the low half follows"):
+                nc.vector.reciprocal(out=mv[:, :, 0:1], in_=sums.unsqueeze(2))
+
+        def low_half(vec, mv):
             nc.vector.tensor_tensor(out=mv[:, :, 1:2], in0=vec.unsqueeze(2), in1=mv[:, :, 0:1],
                                     op=ALU.subtract)
 
         def a_of_p_tiles(lo, hi, sums):
             nc.vector.tensor_reduce(out=s_all[:, lo:hi], in_=sums, axis=AX.X, op=ALU.add)
-            nc.vector.reciprocal(out=a_all[:, lo:hi], in_=s_all[:, lo:hi])
-            split(mva[:, lo:hi, :], a_all[:, lo:hi])
+            inverse_and_halves(a_all[:, lo:hi], mva[:, lo:hi, :], s_all[:, lo:hi])
+            low_half(a_all[:, lo:hi], mva[:, lo:hi, :])
 
         def acc_step(v, h):
             hs = slice(h * 512, (h + 1) * 512)
@@ -266,13 +275,14 @@ def tile_differentiablematcher_t_kernel(tc, pred_masks, gt_masks, out):
                     in1=acc[:, hs], op0=ALU.mult, op1=ALU.add)
 
         def col_open():
-            csp_of[0] = bank(6, [P, CC, 3, NCOL], F32, "csp")
+            for h in range(2):
+                csp_of[h] = bank(6 + h, [P, 4, 2, NCOL], F32, "csp")
 
         def col_pe(jc, g):
             k = 0
             for t in range(g * GT, (g + 1) * GT):
                 for ea in (eah[t], eal[t]):
-                    nc.tensor.matmul(csp_of[0][:, jc, g, :], lhsT=ea[:, jc * P:(jc + 1) * P],
+                    nc.tensor.matmul(csp_of[jc // 4][:, jc % 4, g, :], lhsT=ea[:, jc * P:(jc + 1) * P],
                                      rhs=mva[:, t, :], start=(k == 0), stop=(k == 2 * GT - 1))
                     k += 1
 
@@ -314,92 +324,174 @@ def tile_differentiablematcher_t_kernel(tc, pred_masks, gt_masks, out):
                 col_pe(jc, 0)
                 col_pe(jc, 1)
 
-        acch = big.tile([P, COLS], BF16, name="acch", offset=OFF_ACCH)
-        accl = big.tile([P, COLS], BF16, name="accl", offset=OFF_ACCL)
         junk = big.tile([P, 512], F32, name="junk", offset=OFF_JUNK)
+        sjunk = big.tile([P, 512], BF16, name="sjunk", offset=OFF_SJUNK)
+        bcs = big.tile([P, COLS], F32, name="bcs", offset=OFF_BCS)
+        dm = bank(0, [P, 512], F32, "dm")
+        bc = {}
+        at_of = {}
+        rsp = {}
+        done = {"n": 0}
 
-        def broadcast_bv():
-            bc = []
-            for h in range(2):
-                b = bank(2 + h, [P, 512], F32, "bc")
-                bc.append(b)
-            for jc in range(CC):
-                o = bc[jc // 4][:, (jc % 4) * P:(jc % 4 + 1) * P]
+        def tick(n):
+            done["n"] += n
+            if done["n"] >= TICK:
+                done["n"] = 0
+                for w in BURST:
+                    nc.tensor.matmul_mx(
+                        out=dm[:, 0:w],
+                        lhsT=gc[(0, 0)][:, 0:P].bitcast(FP8X4), lhsT_scale=gs[(0, 0)][:, 0:P],
+                        rhs=gc[(0, 0)][:, 0:w].bitcast(FP8X4), rhs_scale=gs[(0, 0)][:, 0:w],
+                        start=True, stop=True)
+
+        def broadcast(h):
+            bc[h] = bank(2 + h, [P, 512], F32, "bc")
+            for jc in range(4 * h, 4 * h + 4):
+                o = bc[h][:, (jc % 4) * P:(jc % 4 + 1) * P]
                 nc.tensor.transpose(o, bv[:, jc:jc + 1].to_broadcast([P, P]), ident_f[:])
-            return bc
 
-        def col_finish(first_left):
-            csp = csp_of[0]
-            for i in range(first_left, 2 * NV):
-                acc_step(i // 2, i % 2)
-                if i >= 2 * NV - 2:
-                    hs = slice((i % 2) * 512, (i % 2 + 1) * 512)
-                    nc.scalar.copy(out=acch[:, hs], in_=acc[:, hs])
-            if first_left >= 2 * NV:
-                for h in range(2):
-                    nc.scalar.copy(out=acch[:, h * 512:(h + 1) * 512], in_=acc[:, h * 512:(h + 1) * 512])
-            for h in range(2):
-                hs = slice(h * 512, (h + 1) * 512)
-                nc.vector.tensor_tensor(out=accl[:, hs], in0=acc[:, hs], in1=acch[:, hs],
-                                        op=ALU.subtract)
-                for jc in range(4 * h, 4 * h + 4):
-                    nc.tensor.matmul(csp[:, jc, 2, :], lhsT=acch[:, jc * P:(jc + 1) * P],
-                                     rhs=onescol[:], start=True, stop=False)
-                    nc.tensor.matmul(csp[:, jc, 2, :], lhsT=accl[:, jc * P:(jc + 1) * P],
-                                     rhs=onescol[:], start=False, stop=True)
-            nc.vector.tensor_reduce(out=tt[:], in_=csp[:], axis=AX.XY, op=ALU.add)
-            nc.vector.reciprocal(out=bv[:], in_=tt[:])
-            split(mvb, bv[:])
+        def spread(h):
+            nc.scalar.copy(out=bcs[:, h * 512:(h + 1) * 512], in_=bc[h][:])
 
-        def row_phase():
-            bc = broadcast_bv()
-            rsp = [bank(4 + g, [P, GT, NCOL], F32, "rsp") for g in range(2)]
-            for t in range(NP):
+        def rows_pe(h, lo, hi):
+            for t in range(lo, hi):
                 k = 0
-                for jc in range(CC):
+                for jc in range(4 * h, 4 * h + 4):
                     for eb in (ebh[t], ebl[t]):
-                        nc.tensor.matmul(rsp[t // GT][:, t % GT, :], lhsT=eb[:, jc, :],
-                                         rhs=mvb[:, jc, :],
-                                         start=(k == 0), stop=(k == 2 * CC - 1))
+                        nc.tensor.matmul(rsp[t // GT][:, t % GT, h, :], lhsT=eb[:, jc, :],
+                                         rhs=mvb[:, jc, :], start=(k == 0), stop=(k == 7))
                         k += 1
-            for i in range(2 * NV):
-                v = i // 2
-                h = i % 2
-                nc.vector.scalar_tensor_tensor(
-                    out=junk[:], in0=ev[v][:, h * 512:(h + 1) * 512], scalar=1.0,
-                    in1=bc[h][:], op0=ALU.mult, op1=ALU.mult,
-                    accum_out=svh[:, v, h:h + 1])
-                if i == MID - 1:
-                    a_of_p_tiles(0, GT, rsp[0][:])
-            nc.vector.tensor_reduce(out=s_all[:, NP:RT], in_=svh[:], axis=AX.X, op=ALU.add)
-            nc.vector.reciprocal(out=a_all[:, NP:RT], in_=s_all[:, NP:RT])
-            for i in range(EARLY):
-                acc_step(i // 2, i % 2)
-            a_of_p_tiles(GT, NP, rsp[1][:])
+                tick(8)
 
-        def col_phase():
-            col_open()
-            for g in range(2):
-                for jc in range(CC):
-                    col_pe(jc, g)
-            col_finish(EARLY)
+        def cols_pe(g, h):
+            for jc in range(4 * h, 4 * h + 4):
+                col_pe(jc, g)
+                tick(2 * GT)
+
+        def acc_turn(h):
+            at_of[h] = bank(1, [P, 4, P], F32, "at")
+            for j in range(4):
+                jc = 4 * h + j
+                nc.tensor.transpose(at_of[h][:, j, :], acc[:, jc * P:(jc + 1) * P], ident_f[:])
+
+        def acc_sums(h):
+            for j in range(4):
+                jc = 4 * h + j
+                nc.scalar.activation(out=sjunk[:, 0:P], in_=at_of[h][:, j, :], func=ACT.Copy,
+                                     accum_out=acs[:, jc:jc + 1])
+
+        def row_v(v, h):
+            nc.vector.scalar_tensor_tensor(
+                out=junk[:], in0=ev[v][:, h * 512:(h + 1) * 512], scalar=1.0,
+                in1=bc[h][:], op0=ALU.mult, op1=ALU.mult, accum_out=svh[:, v, h:h + 1])
+
+        prod_of = {}
+
+        def row_g(v, h):
+            pr = big.tile([P, 512], F32, name="prod%d" % (v % 2), offset=OFF_GRP + (v % 2) * 2 * KB)
+            hs = slice(h * 512, (h + 1) * 512)
+            nc.gpsimd.tensor_tensor(out=pr[:], in0=ev[v][:, hs], in1=bcs[:, hs], op=ALU.mult)
+            prod_of[(v, h)] = pr
+
+        def row_gsum(v, h):
+            nc.scalar.activation(out=sjunk[:], in_=prod_of[(v, h)][:], func=ACT.Copy,
+                                 accum_out=svh[:, v, h:h + 1])
+
+        def b_steps(h):
+            js = slice(4 * h, 4 * h + 4)
+            return [
+                lambda: nc.vector.tensor_reduce(out=tt[:, js], in_=csp_of[h][:, :, :, 0:2], axis=AX.XY, op=ALU.add),
+                lambda: nc.vector.tensor_tensor(out=tt[:, js], in0=tt[:, js], in1=acs[:, js], op=ALU.add),
+                lambda: inverse_and_halves(bv[:, js], mvb[:, js, :], tt[:, js]),
+                lambda: low_half(bv[:, js], mvb[:, js, :]),
+            ]
+
+        def p_steps(g):
+            ts = slice(g * GT, (g + 1) * GT)
+            return [
+                lambda: nc.vector.tensor_reduce(out=s_all[:, ts], in_=rsp[g][:, :, :, 0:2], axis=AX.XY, op=ALU.add),
+                lambda: inverse_and_halves(a_all[:, ts], mva[:, ts, :], s_all[:, ts]),
+                lambda: low_half(a_all[:, ts], mva[:, ts, :]),
+            ]
+
+        def v_steps(lo, hi):
+            return [
+                lambda: nc.vector.tensor_reduce(out=s_all[:, NP + lo:NP + hi], in_=svh[:, lo:hi, :], axis=AX.X, op=ALU.add),
+                lambda: nc.vector.reciprocal(out=a_all[:, NP + lo:NP + hi], in_=s_all[:, NP + lo:NP + hi]),
+            ]
 
         r32 = {}
-        col_finish(2 * NV)
+        acc_turn(0)
+        acc_sums(0)
+        for f in b_steps(0):
+            f()
         for it in range(1, ITERS):
-            row_phase()
+            broadcast(0)
+            spread(0)
+            for g in range(2):
+                rsp[g] = bank(4 + g, [P, GT, 2, NCOL], F32, "rsp")
+            rows_pe(0, 0, 6)
+            acc_turn(1)
+            acc_sums(1)
+            b1 = b_steps(1)
+            for v in range(VR):
+                row_v(v, 0)
+                if v >= 2:
+                    b1[v - 2]()
+            rows_pe(0, 6, 20)
+            for v in range(VR, NV):
+                row_g(v, 0)
+                row_gsum(v, 0)
+                if v == VR + 1:
+                    broadcast(1)
+                    spread(1)
+            rows_pe(0, 20, NP)
+            for v in range(VR):
+                row_v(v, 1)
+            for v in range(VR, NV):
+                row_g(v, 1)
+                row_gsum(v, 1)
+            rows_pe(1, 0, GT)
+            rows_pe(1, GT, NP)
+            pa = p_steps(0)
+            va = v_steps(0, VR)
+            pa[0]()
+            va[0]()
+            pa[1]()
+            va[1]()
+            pa[2]()
             if it == ITERS - 1:
                 for t in range(0, NP, 2):
                     r = big.tile([P, 2, COLS], F32, name="r32_%d" % t, offset=OFF_EB + t * 4 * KB)
                     if t < NP - REBUILT:
                         nc.sync.dma_start(out=r[:], in_=ov[:, t:t + 2, :])
                     r32[t] = r
-            col_phase()
+            col_open()
+            cols_pe(0, 0)
+            cols_pe(0, 1)
+            extra = dict(zip((1, 2, 3, 4, 5), v_steps(VR, NV) + p_steps(1)))
+            for v in range(NV):
+                acc_step(v, 0)
+                if v in extra:
+                    extra[v]()
+            cols_pe(1, 0)
+            acc_turn(0)
+            acc_sums(0)
+            cols_pe(1, 1)
+            b0 = b_steps(0)
+            for v in range(NV):
+                acc_step(v, 1)
+                if 4 <= v < 8:
+                    b0[v - 4]()
 
-        bc = broadcast_bv()
-        bcs = big.tile([P, COLS], F32, name="bcs", offset=OFF_BCS)
+        acc_turn(1)
+        acc_sums(1)
+        for f in b_steps(1):
+            f()
+
         for h in range(2):
-            nc.scalar.copy(out=bcs[:, h * 512:(h + 1) * 512], in_=bc[h][:])
+            broadcast(h)
+            spread(h)
         g_pairs = [t for t in range(0, NP, 2) if t < 2 * GPAIRS]
         v_pairs = [t for t in range(0, NP - REBUILT, 2) if t >= 2 * GPAIRS]
         r_tiles = list(range(NP - REBUILT, NP))

@@ -20,17 +20,23 @@ RT = ROWS // P
 CC = COLS // P
 NP = 22
 NV = RT - NP
-NCOL = 3
+NCOL = 7
 ITERS = 5
 INV_TEMP = 10.0
 KB = 1024
 VR = 6
-TICK = 64
-BURST = (512, 256, 128)
-GPAIRS = 5
+TICK = 56
+WARM = 4
+GPAIRS = 6
 GT = NP // 2
-REBUILT = 8
-COL_SLOTS = {26: [0], 27: [1], 28: [2], 29: [3], 30: [4], 31: [5], 32: [6, 7]}
+REBUILT = 2
+COL_SLOTS = {31: [(0, 0), (0, 1)],
+             32: [(0, 2), (0, 3), (0, 4), (0, 5), (0, 6), (0, 7)],
+             33: [(1, 0), (1, 1), (1, 2), (1, 3)],
+             34: [(1, 4), (1, 5), (1, 6), (1, 7)]}
+A_SLOTS = (20, 32)
+V_TILES = [4 + 3 * v for v in range(NV)]
+P_TILES = [t for t in range(RT) if t not in V_TILES]
 FLOPS = 2 * ROWS * COLS * CONTR
 
 OFF_EAH = 0
@@ -60,7 +66,7 @@ def tile_differentiablematcher_t_kernel(tc, pred_masks, gt_masks, out):
     with ExitStack() as ctx:
         big = ctx.enter_context(tc.tile_pool(name="big", bufs=1))
         small = ctx.enter_context(tc.tile_pool(name="small", bufs=1))
-        tiny = ctx.enter_context(tc.tile_pool(name="tiny", bufs=4))
+        tiny = ctx.enter_context(tc.tile_pool(name="tiny", bufs=3))
         ps = ctx.enter_context(tc.psum_pool(name="ps", bufs=1))
         ctx.enter_context(tc.manual_schedule())
 
@@ -72,10 +78,8 @@ def tile_differentiablematcher_t_kernel(tc, pred_masks, gt_masks, out):
             nc.sync.dma_start(out=g_raw[:, 2 * q:2 * q + 2, :], in_=gv[:, 2 * q:2 * q + 2, :])
         p_raw = []
         for n in range(RT // 2):
-            if 2 * n < NP:
-                off = OFF_EB + 2 * n * 4 * KB
-            else:
-                off = OFF_EV + (2 * n - NP + 1) * 4 * KB
+            host = 2 * n if 2 * n in P_TILES else 2 * n + 1
+            off = OFF_EB + P_TILES.index(host) * 4 * KB
             r = big.tile([P, 2, CONTR], BF16, name="p_raw%d" % n, offset=off)
             nc.sync.dma_start(out=r[:], in_=pv[:, 2 * n:2 * n + 2, :])
             p_raw.append(r)
@@ -149,15 +153,12 @@ def tile_differentiablematcher_t_kernel(tc, pred_masks, gt_masks, out):
                 lo = 256 * g + u
                 nc.tensor.transpose(tp_of[t][:, g, u, :], src[:, lo:lo + 255:2], ident_f[:])
 
-        def do_regroup(t, on_vector):
+        def do_regroup(t):
             grp = big.tile([P, 4 * 256], BF16, name="grp%d" % (t % 2),
                            offset=OFF_GRP + (t % 2) * 2 * KB, align_bytes=64)
             dst = grp[:].bitcast(F32).rearrange("p (g i u) -> p g i u", g=2, u=2)
             words = tp_of[t][:].rearrange("p g u i -> p g i u")
-            if on_vector:
-                nc.vector.tensor_copy(out=dst, in_=words)
-            else:
-                nc.scalar.copy(out=dst, in_=words)
+            nc.scalar.copy(out=dst, in_=words)
             grp_of[t] = grp
 
         def do_quantise(t):
@@ -190,62 +191,64 @@ def tile_differentiablematcher_t_kernel(tc, pred_masks, gt_masks, out):
                 m2_of[t] = tiny.tile([P, 2], F32, name="m2")
             m2 = m2_of[t]
             nc.vector.tensor_reduce(out=m2[:, h:h + 1], in_=d_of[(t, h)][:], axis=AX.X, op=ALU.max)
-            if h == 1:
-                nb = tiny.tile([P, 1], F32, name="nb")
-                nc.vector.tensor_scalar(out=nb[:], in0=m2[:, 0:1], scalar1=m2[:, 1:2],
-                                        scalar2=-INV_TEMP, op0=ALU.max, op1=ALU.mult)
-                nb_of[t] = nb
+
+        def do_bias(t):
+            m2 = m2_of[t]
+            nb = tiny.tile([P, 1], F32, name="nb")
+            nc.vector.tensor_scalar(out=nb[:], in0=m2[:, 0:1], scalar1=m2[:, 1:2],
+                                    scalar2=-INV_TEMP, op0=ALU.max, op1=ALU.mult)
+            nb_of[t] = nb
 
         def do_exp(t):
             ds = [d_of[(t, 0)], d_of[(t, 1)]]
-            if t < NP:
-                dest = big.tile([P, COLS], F32, name="e32_%d" % (t % 3),
-                                offset=OFF_EV + (4 + 2 * (t % 3)) * 4 * KB)
-                e32_of[t] = dest
+            if t in P_TILES:
+                i = P_TILES.index(t)
+                dest = big.tile([P, COLS], F32, name="e32_%d" % i, offset=OFF_EB + i * 4 * KB)
+                e32_of[i] = dest
+                eah[i] = big.tile([P, COLS], BF16, name="eah%d" % i, offset=OFF_EAH + i * 2 * KB)
+                col = i
             else:
-                dest = big.tile([P, COLS], F32, name="ev%d" % (t - NP),
-                                offset=OFF_EV + (t - NP) * 4 * KB)
-                ev[t - NP] = dest
-            if t < NP:
-                eah[t] = big.tile([P, COLS], BF16, name="eah%d" % t, offset=OFF_EAH + t * 2 * KB)
+                v = V_TILES.index(t)
+                dest = big.tile([P, COLS], F32, name="ev%d" % v, offset=OFF_EV + v * 4 * KB)
+                ev[v] = dest
+                col = NP + v
             for h in range(2):
                 hs = slice(h * 512, (h + 1) * 512)
                 nc.scalar.activation(out=dest[:, hs], in_=ds[h][:], func=ACT.Exp,
                                      bias=nb_of[t][:, 0:1], scale=INV_TEMP,
-                                     accum_out=rs[:, t, h:h + 1])
-                if t < NP:
-                    nc.scalar.activation(out=eah[t][:, hs], in_=ds[h][:], func=ACT.Exp,
+                                     accum_out=rs[:, col, h:h + 1])
+                if col < NP:
+                    nc.scalar.activation(out=eah[col][:, hs], in_=ds[h][:], func=ACT.Exp,
                                          bias=nb_of[t][:, 0:1], scale=INV_TEMP)
-            if t < NP - REBUILT:
+            if col < NP - REBUILT:
                 nc.sync.dma_start(out=ov[:, t, :], in_=dest[:])
 
-        def do_sub(t):
-            lo = big.tile([P, COLS], BF16, name="eal%d" % t, offset=OFF_EAL + t * 2 * KB)
+        def do_sub(i):
+            lo = big.tile([P, COLS], BF16, name="eal%d" % i, offset=OFF_EAL + i * 2 * KB)
             for h in range(2):
                 hs = slice(h * 512, (h + 1) * 512)
-                nc.gpsimd.tensor_tensor(out=lo[:, hs], in0=e32_of[t][:, hs], in1=eah[t][:, hs],
+                nc.gpsimd.tensor_tensor(out=lo[:, hs], in0=e32_of[i][:, hs], in1=eah[i][:, hs],
                                         op=ALU.subtract)
-            eal[t] = lo
+            eal[i] = lo
 
-        def do_eb_transposes(t, part):
-            src = eah[t] if part == 0 else eal[t]
+        def do_eb_transposes(i, part):
+            src = eah[i] if part == 0 else eal[i]
             ebp = bank(6 + part, [P, CC, P], BF16, "ebp")
             for jc in range(CC):
                 nc.tensor.transpose(ebp[:, jc, :], src[:, jc * P:(jc + 1) * P], ident_b[:])
-            ebp_of[(t, part)] = ebp
+            ebp_of[(i, part)] = ebp
 
-        def do_eb_copy(t, lo_on_vector):
-            for part in range(2):
-                eb = big.tile([P, CC, P], BF16, name="eb%d_%d" % (part, t),
-                              offset=OFF_EB + t * 4 * KB + part * 2 * KB)
-                if part == 1 and lo_on_vector:
-                    nc.vector.tensor_copy(out=eb[:], in_=ebp_of[(t, part)][:])
-                else:
-                    nc.scalar.copy(out=eb[:], in_=ebp_of[(t, part)][:])
-                if part == 0:
-                    ebh[t] = eb
-                else:
-                    ebl[t] = eb
+        def do_eb_copy(i, part):
+            eb = big.tile([P, CC, P], BF16, name="eb%d_%d" % (part, i),
+                          offset=OFF_EB + i * 4 * KB + part * 2 * KB)
+            if part == 1 or i % 2 == 0:
+                nc.vector.tensor_copy(out=eb[:], in_=ebp_of[(i, part)][:])
+            else:
+                nc.scalar.copy(out=eb[:], in_=ebp_of[(i, part)][:])
+            if part == 0:
+                ebh[i] = eb
+            else:
+                ebl[i] = eb
 
         acc = big.tile([P, COLS], F32, name="acc", offset=OFF_ACC)
         csp_of = {}
@@ -276,73 +279,84 @@ def tile_differentiablematcher_t_kernel(tc, pred_masks, gt_masks, out):
 
         def col_open():
             for h in range(2):
-                csp_of[h] = bank(6 + h, [P, 4, 2, NCOL], F32, "csp")
+                csp_of[h] = bank(h, [P, 4, 2, NCOL], F32, "csp")
 
-        def col_pe(jc, g):
+        def col_pe(jc, g, width):
             k = 0
             for t in range(g * GT, (g + 1) * GT):
                 for ea in (eah[t], eal[t]):
-                    nc.tensor.matmul(csp_of[jc // 4][:, jc % 4, g, :], lhsT=ea[:, jc * P:(jc + 1) * P],
-                                     rhs=mva[:, t, :], start=(k == 0), stop=(k == 2 * GT - 1))
+                    nc.tensor.matmul(csp_of[jc // 4][:, jc % 4, g, 0:width],
+                                     lhsT=ea[:, jc * P:(jc + 1) * P], rhs=mva[:, t, 0:width],
+                                     start=(k == 0), stop=(k == 2 * GT - 1))
                     k += 1
 
-        for s in range(-3, RT + 2):
-            scalar_full = s <= NP
+        for s in range(-3, RT + 3):
+            late = s - 2
+            v_late = V_TILES.index(late) if late in V_TILES else None
+            back = P_TILES.index(s - 4) if s - 4 in P_TILES else None
             if 0 <= s + 2 < RT:
-                do_regroup(s + 2, scalar_full)
-            if s == NP + 1:
-                a_of_p_tiles(0, NP, rs[:, 0:NP, :])
+                do_regroup(s + 2)
             if 0 <= s - 1 < RT:
                 do_exp(s - 1)
-            if 0 <= s - 2 < NP:
-                do_sub(s - 2)
-            if NP <= s - 2 < RT:
-                t = s - 2
-                nc.vector.tensor_reduce(out=s_all[:, t:t + 1], in_=rs[:, t, :], axis=AX.X, op=ALU.add)
-                nc.vector.reciprocal(out=a_all[:, t:t + 1], in_=s_all[:, t:t + 1])
-                acc_step(t - NP, 0)
-                acc_step(t - NP, 1)
+            if late in P_TILES:
+                do_sub(P_TILES.index(late))
             for h in range(2):
                 if 0 <= s < RT:
                     do_mx(s, h)
-            for h in range(2):
-                if 0 <= s - 4 < NP:
-                    do_eb_transposes(s - 4, h)
-            for h in range(2):
+            if back is not None:
+                for part in range(2):
+                    do_eb_transposes(back, part)
+            for g in range(2):
                 if 0 <= s + 3 < RT:
-                    do_transposes(s + 3, h)
-            for h in range(2):
-                if 0 <= s < RT:
-                    do_max(s, h)
+                    do_transposes(s + 3, g)
+            for g in range(2):
+                if s == A_SLOTS[g]:
+                    a_of_p_tiles(g * GT, (g + 1) * GT, rs[:, g * GT:(g + 1) * GT, :])
+            c = None if v_late is None else slice(NP + v_late, NP + v_late + 1)
+            if c is not None:
+                nc.vector.tensor_reduce(out=s_all[:, c], in_=rs[:, c, :], axis=AX.X, op=ALU.add)
+            if 0 <= s < RT:
+                do_max(s, 0)
+            if c is not None:
+                nc.vector.reciprocal(out=a_all[:, c], in_=s_all[:, c])
+            if 0 <= s < RT:
+                do_max(s, 1)
             if 0 <= s + 2 < RT:
                 do_quantise(s + 2)
-            if 0 <= s - 4 < NP:
-                do_eb_copy(s - 4, scalar_full)
-            for jc in COL_SLOTS.get(s, []):
-                if jc == 0:
+            if 0 <= s < RT:
+                do_bias(s)
+            if c is not None:
+                acc_step(v_late, 0)
+                acc_step(v_late, 1)
+            if back is not None:
+                for part in range(2):
+                    do_eb_copy(back, part)
+            for g, jc in COL_SLOTS.get(s, []):
+                if (g, jc) == (0, 0):
                     col_open()
-                col_pe(jc, 0)
-                col_pe(jc, 1)
+                col_pe(jc, g, 2)
 
         junk = big.tile([P, 512], F32, name="junk", offset=OFF_JUNK)
         sjunk = big.tile([P, 512], BF16, name="sjunk", offset=OFF_SJUNK)
         bcs = big.tile([P, COLS], F32, name="bcs", offset=OFF_BCS)
-        dm = bank(0, [P, 512], F32, "dm")
+        dm = bank(7, [P, 512], F32, "dm")
         bc = {}
         at_of = {}
         rsp = {}
         done = {"n": 0}
 
+        def wide_passes(n):
+            done["n"] = 0
+            for k in range(n):
+                nc.tensor.matmul_mx(
+                    out=dm[:], lhsT=gc[(0, 0)][:, 0:P].bitcast(FP8X4), lhsT_scale=gs[(0, 0)][:, 0:P],
+                    rhs=gc[(0, 0)][:].bitcast(FP8X4), rhs_scale=gs[(0, 0)][:],
+                    start=True, stop=True)
+
         def tick(n):
             done["n"] += n
             if done["n"] >= TICK:
-                done["n"] = 0
-                for w in BURST:
-                    nc.tensor.matmul_mx(
-                        out=dm[:, 0:w],
-                        lhsT=gc[(0, 0)][:, 0:P].bitcast(FP8X4), lhsT_scale=gs[(0, 0)][:, 0:P],
-                        rhs=gc[(0, 0)][:, 0:w].bitcast(FP8X4), rhs_scale=gs[(0, 0)][:, 0:w],
-                        start=True, stop=True)
+                wide_passes(1)
 
         def broadcast(h):
             bc[h] = bank(2 + h, [P, 512], F32, "bc")
@@ -365,11 +379,11 @@ def tile_differentiablematcher_t_kernel(tc, pred_masks, gt_masks, out):
 
         def cols_pe(g, h):
             for jc in range(4 * h, 4 * h + 4):
-                col_pe(jc, g)
+                col_pe(jc, g, NCOL)
                 tick(2 * GT)
 
         def acc_turn(h):
-            at_of[h] = bank(1, [P, 4, P], F32, "at")
+            at_of[h] = bank(6, [P, 4, P], F32, "at")
             for j in range(4):
                 jc = 4 * h + j
                 nc.tensor.transpose(at_of[h][:, j, :], acc[:, jc * P:(jc + 1) * P], ident_f[:])
@@ -397,11 +411,15 @@ def tile_differentiablematcher_t_kernel(tc, pred_masks, gt_masks, out):
             nc.scalar.activation(out=sjunk[:], in_=prod_of[(v, h)][:], func=ACT.Copy,
                                  accum_out=svh[:, v, h:h + 1])
 
-        def b_steps(h):
+        def b_steps(h, last):
             js = slice(4 * h, 4 * h + 4)
-            return [
+            sums = [
                 lambda: nc.vector.tensor_reduce(out=tt[:, js], in_=csp_of[h][:, :, :, 0:2], axis=AX.XY, op=ALU.add),
                 lambda: nc.vector.tensor_tensor(out=tt[:, js], in0=tt[:, js], in1=acs[:, js], op=ALU.add),
+            ]
+            if last:
+                return sums + [lambda: nc.vector.reciprocal(out=bv[:, js], in_=tt[:, js])]
+            return sums + [
                 lambda: inverse_and_halves(bv[:, js], mvb[:, js, :], tt[:, js]),
                 lambda: low_half(bv[:, js], mvb[:, js, :]),
             ]
@@ -421,11 +439,21 @@ def tile_differentiablematcher_t_kernel(tc, pred_masks, gt_masks, out):
             ]
 
         r32 = {}
+        g_pairs = [t for t in range(0, NP, 2) if t < 2 * GPAIRS]
+        v_pairs = [t for t in range(0, NP - REBUILT, 2) if t >= 2 * GPAIRS]
+        r_tiles = list(range(NP - REBUILT, NP))
+
+        def scale_rows(t):
+            for e in range(2):
+                nc.scalar.activation(out=r32[t][:, e, :], in_=r32[t][:, e, :], func=ACT.Copy,
+                                     scale=a_all[:, t + e:t + e + 1])
+
         acc_turn(0)
         acc_sums(0)
-        for f in b_steps(0):
+        for f in b_steps(0, False):
             f()
         for it in range(1, ITERS):
+            wide_passes(WARM)
             broadcast(0)
             spread(0)
             for g in range(2):
@@ -433,7 +461,7 @@ def tile_differentiablematcher_t_kernel(tc, pred_masks, gt_masks, out):
             rows_pe(0, 0, 6)
             acc_turn(1)
             acc_sums(1)
-            b1 = b_steps(1)
+            b1 = b_steps(1, False)
             for v in range(VR):
                 row_v(v, 0)
                 if v >= 2:
@@ -464,7 +492,7 @@ def tile_differentiablematcher_t_kernel(tc, pred_masks, gt_masks, out):
                 for t in range(0, NP, 2):
                     r = big.tile([P, 2, COLS], F32, name="r32_%d" % t, offset=OFF_EB + t * 4 * KB)
                     if t < NP - REBUILT:
-                        nc.sync.dma_start(out=r[:], in_=ov[:, t:t + 2, :])
+                        nc.sync.dma_start(out=r[:], in_=ov[:, P_TILES[t]:P_TILES[t] + 2, :])
                     r32[t] = r
             col_open()
             cols_pe(0, 0)
@@ -476,65 +504,73 @@ def tile_differentiablematcher_t_kernel(tc, pred_masks, gt_masks, out):
                     extra[v]()
             cols_pe(1, 0)
             acc_turn(0)
+            if it == ITERS - 1:
+                for t in g_pairs[0:2]:
+                    scale_rows(t)
             acc_sums(0)
             cols_pe(1, 1)
-            b0 = b_steps(0)
+            b0 = dict(zip((4, 5, 6, 7), b_steps(0, it == ITERS - 1)))
             for v in range(NV):
                 acc_step(v, 1)
-                if 4 <= v < 8:
-                    b0[v - 4]()
+                if v in b0:
+                    b0[v]()
 
-        acc_turn(1)
-        acc_sums(1)
-        for f in b_steps(1):
-            f()
-
-        for h in range(2):
-            broadcast(h)
-            spread(h)
-        g_pairs = [t for t in range(0, NP, 2) if t < 2 * GPAIRS]
-        v_pairs = [t for t in range(0, NP - REBUILT, 2) if t >= 2 * GPAIRS]
-        r_tiles = list(range(NP - REBUILT, NP))
-        sum_banks = [(0, 1), (4, 5), (6, 7)]
+        sum_banks = [(4, 5), (6, 7)]
         sums = {}
 
         def rebuild(i):
             t = r_tiles[i]
             for h in range(2):
                 hs = slice(h * 512, (h + 1) * 512)
-                esum = bank(sum_banks[i % 3][h], [P, 512], F32, "esum")
+                esum = bank(sum_banks[i % 2][h], [P, 512], F32, "esum")
                 nc.tensor.matmul(esum[:], lhsT=ident_b[:], rhs=eah[t][:, hs], start=True, stop=False)
                 nc.tensor.matmul(esum[:], lhsT=ident_b[:], rhs=eal[t][:, hs], start=False, stop=True)
                 sums[(t, h)] = esum
 
-        for i in range(3):
+        def out_v(v, h):
+            hs = slice(h * 512, (h + 1) * 512)
+            nc.vector.scalar_tensor_tensor(
+                out=ev[v][:, hs], in0=ev[v][:, hs], scalar=a_all[:, NP + v:NP + v + 1],
+                in1=bc[h][:], op0=ALU.mult, op1=ALU.mult)
+
+        def out_g(t, e, cols):
+            nc.gpsimd.tensor_tensor(out=r32[t][:, e, cols], in0=r32[t][:, e, cols], in1=bcs[:, cols],
+                                    op=ALU.mult)
+
+        broadcast(0)
+        spread(0)
+        acc_turn(1)
+        acc_sums(1)
+        b1 = b_steps(1, True)
+        for v in range(4):
+            out_v(v, 0)
+            if v >= 1:
+                b1[v - 1]()
+        for e in range(2):
+            out_g(g_pairs[0], e, slice(0, 512))
+        broadcast(1)
+        spread(1)
+        for i in range(2):
             rebuild(i)
+        for t in g_pairs[2:]:
+            scale_rows(t)
         for t in g_pairs:
             for e in range(2):
-                nc.scalar.activation(out=r32[t][:, e, :], in_=r32[t][:, e, :], func=ACT.Copy,
-                                     scale=a_all[:, t + e:t + e + 1])
-        for t in g_pairs:
-            for e in range(2):
-                nc.gpsimd.tensor_tensor(out=r32[t][:, e, :], in0=r32[t][:, e, :], in1=bcs[:],
-                                        op=ALU.mult)
-            nc.scalar.dma_start(out=ov[:, t:t + 2, :], in_=r32[t][:])
+                out_g(t, e, slice(512, COLS) if t == g_pairs[0] else slice(0, COLS))
+            nc.scalar.dma_start(out=ov[:, P_TILES[t]:P_TILES[t] + 2, :], in_=r32[t][:])
         for v in range(NV):
-            for h in range(2):
-                hs = slice(h * 512, (h + 1) * 512)
-                nc.vector.scalar_tensor_tensor(
-                    out=ev[v][:, hs], in0=ev[v][:, hs], scalar=a_all[:, NP + v:NP + v + 1],
-                    in1=bc[h][:], op0=ALU.mult, op1=ALU.mult)
-            nc.sync.dma_start(out=ov[:, NP + v, :], in_=ev[v][:])
+            if v >= 4:
+                out_v(v, 0)
+            out_v(v, 1)
+            nc.sync.dma_start(out=ov[:, V_TILES[v], :], in_=ev[v][:])
         for i, t in enumerate(r_tiles):
             for h in range(2):
                 hs = slice(h * 512, (h + 1) * 512)
                 nc.vector.scalar_tensor_tensor(
                     out=r32[t - t % 2][:, t % 2, hs], in0=sums[(t, h)][:],
                     scalar=a_all[:, t:t + 1], in1=bcs[:, hs], op0=ALU.mult, op1=ALU.mult)
-            if i + 3 < REBUILT:
-                rebuild(i + 3)
             if t % 2 == 1:
-                nc.sync.dma_start(out=ov[:, t - 1:t + 1, :], in_=r32[t - 1][:])
+                nc.sync.dma_start(out=ov[:, P_TILES[t - 1]:P_TILES[t - 1] + 2, :], in_=r32[t - 1][:])
         for t in v_pairs:
             for e in range(2):
                 for h in range(2):
@@ -543,4 +579,4 @@ def tile_differentiablematcher_t_kernel(tc, pred_masks, gt_masks, out):
                         out=r32[t][:, e, hs], in0=r32[t][:, e, hs],
                         scalar=a_all[:, t + e:t + e + 1], in1=bc[h][:],
                         op0=ALU.mult, op1=ALU.mult)
-            nc.sync.dma_start(out=ov[:, t:t + 2, :], in_=r32[t][:])
+            nc.sync.dma_start(out=ov[:, P_TILES[t]:P_TILES[t] + 2, :], in_=r32[t][:])

@@ -25,8 +25,9 @@ ITERS = 5
 INV_TEMP = 10.0
 KB = 1024
 VR = 6
-TICK = 56
+TICK = 48
 WARM = 4
+KEEP = 2
 GPAIRS = 6
 GT = NP // 2
 REBUILT = 2
@@ -380,7 +381,10 @@ def tile_differentiablematcher_t_kernel(tc, pred_masks, gt_masks, out):
         def cols_pe(g, h):
             for jc in range(4 * h, 4 * h + 4):
                 col_pe(jc, g, NCOL)
-                tick(2 * GT)
+                if jc == 0:
+                    wide_passes(KEEP)
+                else:
+                    tick(2 * GT)
 
         def acc_turn(h):
             at_of[h] = bank(6, [P, 4, P], F32, "at")
@@ -453,12 +457,12 @@ def tile_differentiablematcher_t_kernel(tc, pred_masks, gt_masks, out):
         for f in b_steps(0, False):
             f()
         for it in range(1, ITERS):
-            wide_passes(WARM)
             broadcast(0)
+            wide_passes(WARM)
             spread(0)
             for g in range(2):
                 rsp[g] = bank(4 + g, [P, GT, 2, NCOL], F32, "rsp")
-            rows_pe(0, 0, 6)
+            rows_pe(0, 0, 10)
             acc_turn(1)
             acc_sums(1)
             b1 = b_steps(1, False)
@@ -466,7 +470,7 @@ def tile_differentiablematcher_t_kernel(tc, pred_masks, gt_masks, out):
                 row_v(v, 0)
                 if v >= 2:
                     b1[v - 2]()
-            rows_pe(0, 6, 20)
+            rows_pe(0, 10, 20)
             for v in range(VR, NV):
                 row_g(v, 0)
                 row_gsum(v, 0)
@@ -479,6 +483,7 @@ def tile_differentiablematcher_t_kernel(tc, pred_masks, gt_masks, out):
             for v in range(VR, NV):
                 row_g(v, 1)
                 row_gsum(v, 1)
+            wide_passes(KEEP)
             rows_pe(1, 0, GT)
             rows_pe(1, GT, NP)
             pa = p_steps(0)

@@ -18,27 +18,23 @@ COLS = 1024
 CONTR = 1024
 RT = ROWS // P
 CC = COLS // P
-NP = 22
-NV = RT - NP
-NCOL = 7
 ITERS = 5
 INV_TEMP = 10.0
 KB = 1024
-VR = 6
-TICK = 48
-WARM = 4
-KEEP = 2
-GPAIRS = 6
-GT = NP // 2
-REBUILT = 2
-COL_SLOTS = {31: [(0, 0), (0, 1)],
-             32: [(0, 2), (0, 3), (0, 4), (0, 5), (0, 6), (0, 7)],
-             33: [(1, 0), (1, 1), (1, 2), (1, 3)],
-             34: [(1, 4), (1, 5), (1, 6), (1, 7)]}
-A_SLOTS = (20, 32)
+FLOPS = 2 * ROWS * COLS * CONTR
+
+NP = 22
+NV = RT - NP
 V_TILES = [4 + 3 * v for v in range(NV)]
 P_TILES = [t for t in range(RT) if t not in V_TILES]
-FLOPS = 2 * ROWS * COLS * CONTR
+GT = NP // 2
+NCOL = 8
+REBUILT = 1
+VR = 6
+G_OUT = 12
+TICK = 24
+FIRST_A = {20: 0, 32: 1}
+FIRST_COL = {21: [0], 22: [1], 23: [2], 24: [3], 25: [4], 26: [5], 27: [6], 28: [7]}
 
 OFF_EAH = 0
 OFF_EAL = OFF_EAH + NP * 2 * KB
@@ -67,12 +63,20 @@ def tile_differentiablematcher_t_kernel(tc, pred_masks, gt_masks, out):
     with ExitStack() as ctx:
         big = ctx.enter_context(tc.tile_pool(name="big", bufs=1))
         small = ctx.enter_context(tc.tile_pool(name="small", bufs=1))
-        tiny = ctx.enter_context(tc.tile_pool(name="tiny", bufs=3))
+        tiny = ctx.enter_context(tc.tile_pool(name="tiny", bufs=2))
         ps = ctx.enter_context(tc.psum_pool(name="ps", bufs=1))
         ctx.enter_context(tc.manual_schedule())
 
         def bank(b, shape, dtype, name):
             return ps.tile(shape, dtype, name=name, tag="bk%d" % b)
+
+        def col_of(t):
+            return P_TILES.index(t) if t in P_TILES else NP + V_TILES.index(t)
+
+        def e32_offset(t):
+            if t in P_TILES:
+                return OFF_EB + P_TILES.index(t) * 4 * KB
+            return OFF_EV + V_TILES.index(t) * 4 * KB
 
         g_raw = big.tile([P, CC, CONTR], BF16, name="g_raw", offset=OFF_GRAW)
         for q in range(4):
@@ -80,8 +84,7 @@ def tile_differentiablematcher_t_kernel(tc, pred_masks, gt_masks, out):
         p_raw = []
         for n in range(RT // 2):
             host = 2 * n if 2 * n in P_TILES else 2 * n + 1
-            off = OFF_EB + P_TILES.index(host) * 4 * KB
-            r = big.tile([P, 2, CONTR], BF16, name="p_raw%d" % n, offset=off)
+            r = big.tile([P, 2, CONTR], BF16, name="p_raw%d" % n, offset=e32_offset(host))
             nc.sync.dma_start(out=r[:], in_=pv[:, 2 * n:2 * n + 2, :])
             p_raw.append(r)
 
@@ -132,34 +135,32 @@ def tile_differentiablematcher_t_kernel(tc, pred_masks, gt_masks, out):
                     in_=g_grp[:, g, half * 2048:(half + 1) * 2048],
                 )
 
+        tp_of = {}
         grp_of = {}
         cod_of = {}
         d_of = {}
+        m2_of = {}
         nb_of = {}
-        e32_of = {}
-        eah = {}
-        eal = {}
+        e32 = {}
+        ehi = {}
+        elo = {}
         ebp_of = {}
         ebh = {}
         ebl = {}
-        ev = {}
 
-        tp_of = {}
-
-        def do_transposes(t, g):
+        def do_transposes(t):
             src = p_raw[t // 2][:, t % 2, :].bitcast(F32)
-            if g == 0:
-                tp_of[t] = bank(t % 2, [P, 2, 2, P], F32, "tp")
-            for u in range(2):
-                lo = 256 * g + u
-                nc.tensor.transpose(tp_of[t][:, g, u, :], src[:, lo:lo + 255:2], ident_f[:])
+            tp_of[t] = bank(0, [P, 2, 2, P], F32, "tp")
+            for g in range(2):
+                for u in range(2):
+                    lo = 256 * g + u
+                    nc.tensor.transpose(tp_of[t][:, g, u, :], src[:, lo:lo + 255:2], ident_f[:])
 
         def do_regroup(t):
             grp = big.tile([P, 4 * 256], BF16, name="grp%d" % (t % 2),
                            offset=OFF_GRP + (t % 2) * 2 * KB, align_bytes=64)
-            dst = grp[:].bitcast(F32).rearrange("p (g i u) -> p g i u", g=2, u=2)
-            words = tp_of[t][:].rearrange("p g u i -> p g i u")
-            nc.scalar.copy(out=dst, in_=words)
+            nc.scalar.copy(out=grp[:].bitcast(F32).rearrange("p (g i u) -> p g i u", g=2, u=2),
+                           in_=tp_of[t][:].rearrange("p g u i -> p g i u"))
             grp_of[t] = grp
 
         def do_quantise(t):
@@ -185,13 +186,10 @@ def tile_differentiablematcher_t_kernel(tc, pred_masks, gt_masks, out):
                 )
             d_of[(t, h)] = d
 
-        m2_of = {}
-
         def do_max(t, h):
             if h == 0:
                 m2_of[t] = tiny.tile([P, 2], F32, name="m2")
-            m2 = m2_of[t]
-            nc.vector.tensor_reduce(out=m2[:, h:h + 1], in_=d_of[(t, h)][:], axis=AX.X, op=ALU.max)
+            nc.vector.tensor_reduce(out=m2_of[t][:, h:h + 1], in_=d_of[(t, h)][:], axis=AX.X, op=ALU.max)
 
         def do_bias(t):
             m2 = m2_of[t]
@@ -201,60 +199,51 @@ def tile_differentiablematcher_t_kernel(tc, pred_masks, gt_masks, out):
             nb_of[t] = nb
 
         def do_exp(t):
-            ds = [d_of[(t, 0)], d_of[(t, 1)]]
-            if t in P_TILES:
-                i = P_TILES.index(t)
-                dest = big.tile([P, COLS], F32, name="e32_%d" % i, offset=OFF_EB + i * 4 * KB)
-                e32_of[i] = dest
-                eah[i] = big.tile([P, COLS], BF16, name="eah%d" % i, offset=OFF_EAH + i * 2 * KB)
-                col = i
-            else:
-                v = V_TILES.index(t)
-                dest = big.tile([P, COLS], F32, name="ev%d" % v, offset=OFF_EV + v * 4 * KB)
-                ev[v] = dest
-                col = NP + v
+            c = col_of(t)
+            e32[c] = big.tile([P, COLS], F32, name="e32_%d" % c, offset=e32_offset(t))
+            if c < NP:
+                ehi[c] = big.tile([P, COLS], BF16, name="eah%d" % c, offset=OFF_EAH + c * 2 * KB)
             for h in range(2):
                 hs = slice(h * 512, (h + 1) * 512)
-                nc.scalar.activation(out=dest[:, hs], in_=ds[h][:], func=ACT.Exp,
+                nc.scalar.activation(out=e32[c][:, hs], in_=d_of[(t, h)][:], func=ACT.Exp,
                                      bias=nb_of[t][:, 0:1], scale=INV_TEMP,
-                                     accum_out=rs[:, col, h:h + 1])
-                if col < NP:
-                    nc.scalar.activation(out=eah[col][:, hs], in_=ds[h][:], func=ACT.Exp,
+                                     accum_out=rs[:, c, h:h + 1])
+                if c < NP:
+                    nc.scalar.activation(out=ehi[c][:, hs], in_=d_of[(t, h)][:], func=ACT.Exp,
                                          bias=nb_of[t][:, 0:1], scale=INV_TEMP)
-            if col < NP - REBUILT:
-                nc.sync.dma_start(out=ov[:, t, :], in_=dest[:])
+            if c < NP - REBUILT:
+                nc.sync.dma_start(out=ov[:, t, :], in_=e32[c][:])
 
-        def do_sub(i):
-            lo = big.tile([P, COLS], BF16, name="eal%d" % i, offset=OFF_EAL + i * 2 * KB)
+        def do_sub(c):
+            elo[c] = big.tile([P, COLS], BF16, name="elo%d" % c, offset=OFF_EAL + c * 2 * KB)
             for h in range(2):
                 hs = slice(h * 512, (h + 1) * 512)
-                nc.gpsimd.tensor_tensor(out=lo[:, hs], in0=e32_of[i][:, hs], in1=eah[i][:, hs],
+                nc.gpsimd.tensor_tensor(out=elo[c][:, hs], in0=e32[c][:, hs], in1=ehi[c][:, hs],
                                         op=ALU.subtract)
-            eal[i] = lo
 
-        def do_eb_transposes(i, part):
-            src = eah[i] if part == 0 else eal[i]
-            ebp = bank(6 + part, [P, CC, P], BF16, "ebp")
+        def do_eb_transposes(c, part, b):
+            src = ehi[c] if part == 0 else elo[c]
+            ebp = bank(b, [P, CC, P], BF16, "ebp")
             for jc in range(CC):
                 nc.tensor.transpose(ebp[:, jc, :], src[:, jc * P:(jc + 1) * P], ident_b[:])
-            ebp_of[(i, part)] = ebp
+            ebp_of[(c, part)] = ebp
 
-        def do_eb_copy(i, part):
-            eb = big.tile([P, CC, P], BF16, name="eb%d_%d" % (part, i),
-                          offset=OFF_EB + i * 4 * KB + part * 2 * KB)
-            if part == 1 or i % 2 == 0:
-                nc.vector.tensor_copy(out=eb[:], in_=ebp_of[(i, part)][:])
+        def do_eb_copy(c, part, on_vector):
+            eb = big.tile([P, CC, P], BF16, name="eb%d_%d" % (part, c),
+                          offset=OFF_EB + c * 4 * KB + part * 2 * KB)
+            if on_vector:
+                nc.vector.tensor_copy(out=eb[:], in_=ebp_of[(c, part)][:])
             else:
-                nc.scalar.copy(out=eb[:], in_=ebp_of[(i, part)][:])
+                nc.scalar.copy(out=eb[:], in_=ebp_of[(c, part)][:])
             if part == 0:
-                ebh[i] = eb
+                ebh[c] = eb
             else:
-                ebl[i] = eb
+                ebl[c] = eb
 
         acc = big.tile([P, COLS], F32, name="acc", offset=OFF_ACC)
         csp_of = {}
 
-        def inverse_and_halves(vec, mv, sums):
+        def inverse_and_high(vec, mv, sums):
             nc.vector.reciprocal(out=vec, in_=sums)
             with nc.allow_low_precision(reason="the high half; the low half follows"):
                 nc.vector.reciprocal(out=mv[:, :, 0:1], in_=sums.unsqueeze(2))
@@ -263,38 +252,29 @@ def tile_differentiablematcher_t_kernel(tc, pred_masks, gt_masks, out):
             nc.vector.tensor_tensor(out=mv[:, :, 1:2], in0=vec.unsqueeze(2), in1=mv[:, :, 0:1],
                                     op=ALU.subtract)
 
-        def a_of_p_tiles(lo, hi, sums):
-            nc.vector.tensor_reduce(out=s_all[:, lo:hi], in_=sums, axis=AX.X, op=ALU.add)
-            inverse_and_halves(a_all[:, lo:hi], mva[:, lo:hi, :], s_all[:, lo:hi])
-            low_half(a_all[:, lo:hi], mva[:, lo:hi, :])
-
         def acc_step(v, h):
             hs = slice(h * 512, (h + 1) * 512)
             if v == 0:
-                nc.vector.tensor_scalar(out=acc[:, hs], in0=ev[v][:, hs],
+                nc.vector.tensor_scalar(out=acc[:, hs], in0=e32[NP + v][:, hs],
                                         scalar1=a_all[:, NP:NP + 1], scalar2=None, op0=ALU.mult)
             else:
                 nc.vector.scalar_tensor_tensor(
-                    out=acc[:, hs], in0=ev[v][:, hs], scalar=a_all[:, NP + v:NP + v + 1],
+                    out=acc[:, hs], in0=e32[NP + v][:, hs], scalar=a_all[:, NP + v:NP + v + 1],
                     in1=acc[:, hs], op0=ALU.mult, op1=ALU.add)
-
-        def col_open():
-            for h in range(2):
-                csp_of[h] = bank(h, [P, 4, 2, NCOL], F32, "csp")
 
         def col_pe(jc, g, width):
             k = 0
-            for t in range(g * GT, (g + 1) * GT):
-                for ea in (eah[t], eal[t]):
+            for c in range(g * GT, (g + 1) * GT):
+                for ea in (ehi[c], elo[c]):
                     nc.tensor.matmul(csp_of[jc // 4][:, jc % 4, g, 0:width],
-                                     lhsT=ea[:, jc * P:(jc + 1) * P], rhs=mva[:, t, 0:width],
+                                     lhsT=ea[:, jc * P:(jc + 1) * P], rhs=mva[:, c, 0:width],
                                      start=(k == 0), stop=(k == 2 * GT - 1))
                     k += 1
 
-        for s in range(-3, RT + 3):
+        for s in range(-3, RT + 2):
             late = s - 2
             v_late = V_TILES.index(late) if late in V_TILES else None
-            back = P_TILES.index(s - 4) if s - 4 in P_TILES else None
+            back = P_TILES.index(s - 4) if s - 4 in P_TILES[:NP - 2] else None
             if 0 <= s + 2 < RT:
                 do_regroup(s + 2)
             if 0 <= s - 1 < RT:
@@ -306,13 +286,15 @@ def tile_differentiablematcher_t_kernel(tc, pred_masks, gt_masks, out):
                     do_mx(s, h)
             if back is not None:
                 for part in range(2):
-                    do_eb_transposes(back, part)
-            for g in range(2):
-                if 0 <= s + 3 < RT:
-                    do_transposes(s + 3, g)
-            for g in range(2):
-                if s == A_SLOTS[g]:
-                    a_of_p_tiles(g * GT, (g + 1) * GT, rs[:, g * GT:(g + 1) * GT, :])
+                    do_eb_transposes(back, part, 6 + part)
+            if 0 <= s + 3 < RT:
+                do_transposes(s + 3)
+            if s in FIRST_A:
+                lo = FIRST_A[s] * GT
+                hi = lo + GT
+                nc.vector.tensor_reduce(out=s_all[:, lo:hi], in_=rs[:, lo:hi, :], axis=AX.X, op=ALU.add)
+                inverse_and_high(a_all[:, lo:hi], mva[:, lo:hi, :], s_all[:, lo:hi])
+                low_half(a_all[:, lo:hi], mva[:, lo:hi, :])
             c = None if v_late is None else slice(NP + v_late, NP + v_late + 1)
             if c is not None:
                 nc.vector.tensor_reduce(out=s_all[:, c], in_=rs[:, c, :], axis=AX.X, op=ALU.add)
@@ -331,11 +313,13 @@ def tile_differentiablematcher_t_kernel(tc, pred_masks, gt_masks, out):
                 acc_step(v_late, 1)
             if back is not None:
                 for part in range(2):
-                    do_eb_copy(back, part)
-            for g, jc in COL_SLOTS.get(s, []):
-                if (g, jc) == (0, 0):
-                    col_open()
-                col_pe(jc, g, 2)
+                    do_eb_copy(back, part, part == 1 or back % 2 == 0)
+            for jc in FIRST_COL.get(s, []):
+                if jc == 0:
+                    csp = bank(1, [P, 2, 4, 2, 2], F32, "csp")
+                    csp_of[0] = csp[:, 0]
+                    csp_of[1] = csp[:, 1]
+                col_pe(jc, 0, 2)
 
         junk = big.tile([P, 512], F32, name="junk", offset=OFF_JUNK)
         sjunk = big.tile([P, 512], BF16, name="sjunk", offset=OFF_SJUNK)
@@ -344,36 +328,36 @@ def tile_differentiablematcher_t_kernel(tc, pred_masks, gt_masks, out):
         bc = {}
         at_of = {}
         rsp = {}
+        prod_of = {}
         done = {"n": 0}
 
-        def wide_passes(n):
+        def wide_passes(n, width):
             done["n"] = 0
             for k in range(n):
                 nc.tensor.matmul_mx(
-                    out=dm[:], lhsT=gc[(0, 0)][:, 0:P].bitcast(FP8X4), lhsT_scale=gs[(0, 0)][:, 0:P],
-                    rhs=gc[(0, 0)][:].bitcast(FP8X4), rhs_scale=gs[(0, 0)][:],
+                    out=dm[:, 0:width],
+                    lhsT=gc[(0, 0)][:, 0:P].bitcast(FP8X4), lhsT_scale=gs[(0, 0)][:, 0:P],
+                    rhs=gc[(0, 0)][:, 0:width].bitcast(FP8X4), rhs_scale=gs[(0, 0)][:, 0:width],
                     start=True, stop=True)
 
         def tick(n):
             done["n"] += n
             if done["n"] >= TICK:
-                wide_passes(1)
+                wide_passes(1, 256)
 
         def broadcast(h):
             bc[h] = bank(2 + h, [P, 512], F32, "bc")
             for jc in range(4 * h, 4 * h + 4):
                 o = bc[h][:, (jc % 4) * P:(jc % 4 + 1) * P]
                 nc.tensor.transpose(o, bv[:, jc:jc + 1].to_broadcast([P, P]), ident_f[:])
-
-        def spread(h):
             nc.scalar.copy(out=bcs[:, h * 512:(h + 1) * 512], in_=bc[h][:])
 
         def rows_pe(h, lo, hi):
-            for t in range(lo, hi):
+            for c in range(lo, hi):
                 k = 0
                 for jc in range(4 * h, 4 * h + 4):
-                    for eb in (ebh[t], ebl[t]):
-                        nc.tensor.matmul(rsp[t // GT][:, t % GT, h, :], lhsT=eb[:, jc, :],
+                    for eb in (ebh[c], ebl[c]):
+                        nc.tensor.matmul(rsp[c // GT][:, c % GT, h, :], lhsT=eb[:, jc, :],
                                          rhs=mvb[:, jc, :], start=(k == 0), stop=(k == 7))
                         k += 1
                 tick(8)
@@ -381,18 +365,13 @@ def tile_differentiablematcher_t_kernel(tc, pred_masks, gt_masks, out):
         def cols_pe(g, h):
             for jc in range(4 * h, 4 * h + 4):
                 col_pe(jc, g, NCOL)
-                if jc == 0:
-                    wide_passes(KEEP)
-                else:
-                    tick(2 * GT)
+                tick(2 * GT)
 
         def acc_turn(h):
             at_of[h] = bank(6, [P, 4, P], F32, "at")
             for j in range(4):
                 jc = 4 * h + j
                 nc.tensor.transpose(at_of[h][:, j, :], acc[:, jc * P:(jc + 1) * P], ident_f[:])
-
-        def acc_sums(h):
             for j in range(4):
                 jc = 4 * h + j
                 nc.scalar.activation(out=sjunk[:, 0:P], in_=at_of[h][:, j, :], func=ACT.Copy,
@@ -400,15 +379,13 @@ def tile_differentiablematcher_t_kernel(tc, pred_masks, gt_masks, out):
 
         def row_v(v, h):
             nc.vector.scalar_tensor_tensor(
-                out=junk[:], in0=ev[v][:, h * 512:(h + 1) * 512], scalar=1.0,
+                out=junk[:], in0=e32[NP + v][:, h * 512:(h + 1) * 512], scalar=1.0,
                 in1=bc[h][:], op0=ALU.mult, op1=ALU.mult, accum_out=svh[:, v, h:h + 1])
-
-        prod_of = {}
 
         def row_g(v, h):
             pr = big.tile([P, 512], F32, name="prod%d" % (v % 2), offset=OFF_GRP + (v % 2) * 2 * KB)
             hs = slice(h * 512, (h + 1) * 512)
-            nc.gpsimd.tensor_tensor(out=pr[:], in0=ev[v][:, hs], in1=bcs[:, hs], op=ALU.mult)
+            nc.gpsimd.tensor_tensor(out=pr[:], in0=e32[NP + v][:, hs], in1=bcs[:, hs], op=ALU.mult)
             prod_of[(v, h)] = pr
 
         def row_gsum(v, h):
@@ -418,170 +395,157 @@ def tile_differentiablematcher_t_kernel(tc, pred_masks, gt_masks, out):
         def b_steps(h, last):
             js = slice(4 * h, 4 * h + 4)
             sums = [
-                lambda: nc.vector.tensor_reduce(out=tt[:, js], in_=csp_of[h][:, :, :, 0:2], axis=AX.XY, op=ALU.add),
+                lambda: nc.vector.tensor_reduce(out=tt[:, js], in_=csp_of[h][:, :, :, 0:2],
+                                                axis=AX.XY, op=ALU.add),
                 lambda: nc.vector.tensor_tensor(out=tt[:, js], in0=tt[:, js], in1=acs[:, js], op=ALU.add),
             ]
             if last:
                 return sums + [lambda: nc.vector.reciprocal(out=bv[:, js], in_=tt[:, js])]
             return sums + [
-                lambda: inverse_and_halves(bv[:, js], mvb[:, js, :], tt[:, js]),
+                lambda: inverse_and_high(bv[:, js], mvb[:, js, :], tt[:, js]),
                 lambda: low_half(bv[:, js], mvb[:, js, :]),
             ]
 
         def p_steps(g):
-            ts = slice(g * GT, (g + 1) * GT)
+            cs = slice(g * GT, (g + 1) * GT)
             return [
-                lambda: nc.vector.tensor_reduce(out=s_all[:, ts], in_=rsp[g][:, :, :, 0:2], axis=AX.XY, op=ALU.add),
-                lambda: inverse_and_halves(a_all[:, ts], mva[:, ts, :], s_all[:, ts]),
-                lambda: low_half(a_all[:, ts], mva[:, ts, :]),
+                lambda: nc.vector.tensor_reduce(out=s_all[:, cs], in_=rsp[g][:, :, :, 0:2],
+                                                axis=AX.XY, op=ALU.add),
+                lambda: inverse_and_high(a_all[:, cs], mva[:, cs, :], s_all[:, cs]),
+                lambda: low_half(a_all[:, cs], mva[:, cs, :]),
             ]
 
         def v_steps(lo, hi):
+            cs = slice(NP + lo, NP + hi)
             return [
-                lambda: nc.vector.tensor_reduce(out=s_all[:, NP + lo:NP + hi], in_=svh[:, lo:hi, :], axis=AX.X, op=ALU.add),
-                lambda: nc.vector.reciprocal(out=a_all[:, NP + lo:NP + hi], in_=s_all[:, NP + lo:NP + hi]),
+                lambda: nc.vector.tensor_reduce(out=s_all[:, cs], in_=svh[:, lo:hi, :],
+                                                axis=AX.X, op=ALU.add),
+                lambda: nc.vector.reciprocal(out=a_all[:, cs], in_=s_all[:, cs]),
             ]
 
         r32 = {}
-        g_pairs = [t for t in range(0, NP, 2) if t < 2 * GPAIRS]
-        v_pairs = [t for t in range(0, NP - REBUILT, 2) if t >= 2 * GPAIRS]
-        r_tiles = list(range(NP - REBUILT, NP))
 
-        def scale_rows(t):
-            for e in range(2):
-                nc.scalar.activation(out=r32[t][:, e, :], in_=r32[t][:, e, :], func=ACT.Copy,
-                                     scale=a_all[:, t + e:t + e + 1])
+        def scale_rows(c):
+            nc.scalar.activation(out=r32[c][:], in_=r32[c][:], func=ACT.Copy, scale=a_all[:, c:c + 1])
 
+        for jc in range(CC):
+            col_pe(jc, 1, 2)
         acc_turn(0)
-        acc_sums(0)
+        for i in range(2):
+            for part in range(2):
+                do_eb_transposes(NP - 2 + i, part, 2 + 2 * i + part)
+        for i in range(2):
+            do_eb_copy(NP - 2 + i, 0, False)
         for f in b_steps(0, False):
             f()
+        for i in range(2):
+            do_eb_copy(NP - 2 + i, 1, True)
+
         for it in range(1, ITERS):
+            last = it == ITERS - 1
             broadcast(0)
-            wide_passes(WARM)
-            spread(0)
+            wide_passes(4, 512)
             for g in range(2):
                 rsp[g] = bank(4 + g, [P, GT, 2, NCOL], F32, "rsp")
-            rows_pe(0, 0, 10)
+            rows_pe(0, 0, 9)
             acc_turn(1)
-            acc_sums(1)
-            b1 = b_steps(1, False)
+            b1 = dict(zip((2, 3, 4, 5), b_steps(1, False)))
             for v in range(VR):
                 row_v(v, 0)
-                if v >= 2:
-                    b1[v - 2]()
-            rows_pe(0, 10, 20)
+                if v in b1:
+                    b1[v]()
+            rows_pe(0, 9, 20)
             for v in range(VR, NV):
                 row_g(v, 0)
                 row_gsum(v, 0)
                 if v == VR + 1:
                     broadcast(1)
-                    spread(1)
             rows_pe(0, 20, NP)
-            for v in range(VR):
-                row_v(v, 1)
             for v in range(VR, NV):
                 row_g(v, 1)
                 row_gsum(v, 1)
-            wide_passes(KEEP)
-            rows_pe(1, 0, GT)
-            rows_pe(1, GT, NP)
-            pa = p_steps(0)
-            va = v_steps(0, VR)
-            pa[0]()
-            va[0]()
-            pa[1]()
-            va[1]()
-            pa[2]()
-            if it == ITERS - 1:
-                for t in range(0, NP, 2):
-                    r = big.tile([P, 2, COLS], F32, name="r32_%d" % t, offset=OFF_EB + t * 4 * KB)
-                    if t < NP - REBUILT:
-                        nc.sync.dma_start(out=r[:], in_=ov[:, P_TILES[t]:P_TILES[t] + 2, :])
-                    r32[t] = r
-            col_open()
-            cols_pe(0, 0)
-            cols_pe(0, 1)
-            extra = dict(zip((1, 2, 3, 4, 5), v_steps(VR, NV) + p_steps(1)))
+            rows_pe(1, 0, NP)
+            first = dict(zip((4, 5), v_steps(0, 4)))
+            for v in range(VR):
+                row_v(v, 1)
+                if v in first:
+                    first[v]()
+            if last:
+                for c in range(NP):
+                    r32[c] = big.tile([P, COLS], F32, name="r32_%d" % c, offset=OFF_EB + c * 4 * KB)
+                    if c < NP - REBUILT:
+                        nc.sync.dma_start(out=r32[c][:], in_=ov[:, P_TILES[c], :])
+            extra = {}
+            for v, f in zip((0, 1, 2), p_steps(0)):
+                extra[v] = [f]
+            for v, f in zip((1, 2), v_steps(4, VR)):
+                extra[v] = extra[v] + [f]
+            for v, f in zip((3, 4), v_steps(VR, NV)):
+                extra[v] = [f]
+            for v, f in zip((5, 6, 7), p_steps(1)):
+                extra[v] = [f]
             for v in range(NV):
                 acc_step(v, 0)
-                if v in extra:
-                    extra[v]()
+                for f in extra.get(v, []):
+                    f()
+            for h in range(2):
+                csp_of[h] = bank(h, [P, 4, 2, NCOL], F32, "csp")
+            cols_pe(0, 0)
+            cols_pe(0, 1)
             cols_pe(1, 0)
             acc_turn(0)
-            if it == ITERS - 1:
-                for t in g_pairs[0:2]:
-                    scale_rows(t)
-            acc_sums(0)
             cols_pe(1, 1)
-            b0 = dict(zip((4, 5, 6, 7), b_steps(0, it == ITERS - 1)))
+            b0 = dict(zip((4, 5, 6, 7), b_steps(0, last)))
             for v in range(NV):
                 acc_step(v, 1)
                 if v in b0:
                     b0[v]()
-
-        sum_banks = [(4, 5), (6, 7)]
-        sums = {}
-
-        def rebuild(i):
-            t = r_tiles[i]
-            for h in range(2):
-                hs = slice(h * 512, (h + 1) * 512)
-                esum = bank(sum_banks[i % 2][h], [P, 512], F32, "esum")
-                nc.tensor.matmul(esum[:], lhsT=ident_b[:], rhs=eah[t][:, hs], start=True, stop=False)
-                nc.tensor.matmul(esum[:], lhsT=ident_b[:], rhs=eal[t][:, hs], start=False, stop=True)
-                sums[(t, h)] = esum
+            if last:
+                for c in range(3):
+                    scale_rows(c)
 
         def out_v(v, h):
             hs = slice(h * 512, (h + 1) * 512)
             nc.vector.scalar_tensor_tensor(
-                out=ev[v][:, hs], in0=ev[v][:, hs], scalar=a_all[:, NP + v:NP + v + 1],
+                out=e32[NP + v][:, hs], in0=e32[NP + v][:, hs], scalar=a_all[:, NP + v:NP + v + 1],
                 in1=bc[h][:], op0=ALU.mult, op1=ALU.mult)
 
-        def out_g(t, e, cols):
-            nc.gpsimd.tensor_tensor(out=r32[t][:, e, cols], in0=r32[t][:, e, cols], in1=bcs[:, cols],
+        def out_g(c, cols):
+            nc.gpsimd.tensor_tensor(out=r32[c][:, cols], in0=r32[c][:, cols], in1=bcs[:, cols],
                                     op=ALU.mult)
 
         broadcast(0)
-        spread(0)
         acc_turn(1)
-        acc_sums(1)
         b1 = b_steps(1, True)
         for v in range(4):
             out_v(v, 0)
             if v >= 1:
                 b1[v - 1]()
-        for e in range(2):
-            out_g(g_pairs[0], e, slice(0, 512))
+        for c in range(2):
+            out_g(c, slice(0, 512))
         broadcast(1)
-        spread(1)
-        for i in range(2):
-            rebuild(i)
-        for t in g_pairs[2:]:
-            scale_rows(t)
-        for t in g_pairs:
-            for e in range(2):
-                out_g(t, e, slice(512, COLS) if t == g_pairs[0] else slice(0, COLS))
-            nc.scalar.dma_start(out=ov[:, P_TILES[t]:P_TILES[t] + 2, :], in_=r32[t][:])
+        esum = {}
+        for h in range(2):
+            hs = slice(h * 512, (h + 1) * 512)
+            c = NP - 1
+            esum[h] = bank(4 + h, [P, 512], F32, "esum")
+            nc.tensor.matmul(esum[h][:], lhsT=ident_b[:], rhs=ehi[c][:, hs], start=True, stop=False)
+            nc.tensor.matmul(esum[h][:], lhsT=ident_b[:], rhs=elo[c][:, hs], start=False, stop=True)
+        for c in range(3, G_OUT):
+            scale_rows(c)
+        for c in range(G_OUT):
+            out_g(c, slice(512, COLS) if c < 2 else slice(0, COLS))
+            nc.scalar.dma_start(out=ov[:, P_TILES[c], :], in_=r32[c][:])
         for v in range(NV):
             if v >= 4:
                 out_v(v, 0)
             out_v(v, 1)
-            nc.sync.dma_start(out=ov[:, V_TILES[v], :], in_=ev[v][:])
-        for i, t in enumerate(r_tiles):
+            nc.sync.dma_start(out=ov[:, V_TILES[v], :], in_=e32[NP + v][:])
+        for c in [NP - 1] + list(range(G_OUT, NP - 1)):
             for h in range(2):
                 hs = slice(h * 512, (h + 1) * 512)
                 nc.vector.scalar_tensor_tensor(
-                    out=r32[t - t % 2][:, t % 2, hs], in0=sums[(t, h)][:],
-                    scalar=a_all[:, t:t + 1], in1=bcs[:, hs], op0=ALU.mult, op1=ALU.mult)
-            if t % 2 == 1:
-                nc.sync.dma_start(out=ov[:, P_TILES[t - 1]:P_TILES[t - 1] + 2, :], in_=r32[t - 1][:])
-        for t in v_pairs:
-            for e in range(2):
-                for h in range(2):
-                    hs = slice(h * 512, (h + 1) * 512)
-                    nc.vector.scalar_tensor_tensor(
-                        out=r32[t][:, e, hs], in0=r32[t][:, e, hs],
-                        scalar=a_all[:, t + e:t + e + 1], in1=bc[h][:],
-                        op0=ALU.mult, op1=ALU.mult)
-            nc.sync.dma_start(out=ov[:, P_TILES[t]:P_TILES[t] + 2, :], in_=r32[t][:])
+                    out=r32[c][:, hs], in0=esum[h][:] if c == NP - 1 else r32[c][:, hs],
+                    scalar=a_all[:, c:c + 1], in1=bcs[:, hs] if c == NP - 1 else bc[h][:],
+                    op0=ALU.mult, op1=ALU.mult)
+            nc.sync.dma_start(out=ov[:, P_TILES[c], :], in_=r32[c][:])

@@ -23,16 +23,14 @@ INV_TEMP = 10.0
 KB = 1024
 FLOPS = 2 * ROWS * COLS * CONTR
 
-NP = 22
-NV = RT - NP
-V_TILES = [4 + 3 * v for v in range(NV)]
+NV = 13
+NP = RT - NV
+V_TILES = [t for t in range(RT) if (NV * t + 20) % RT < NV]
 P_TILES = [t for t in range(RT) if t not in V_TILES]
-GT = NP // 2
-NCOL = 8
-REBUILT = 1
-VR = 6
-G_OUT = 12
-TICK = 24
+P_PARTS = [(0, 10), (10, NP)]
+NCOL = 2
+REBUILT = 8
+VR = 8
 FIRST_A = {20: 0, 32: 1}
 FIRST_COL = {21: [0], 22: [1], 23: [2], 24: [3], 25: [4], 26: [5], 27: [6], 28: [7]}
 
@@ -83,8 +81,7 @@ def tile_differentiablematcher_t_kernel(tc, pred_masks, gt_masks, out):
             nc.sync.dma_start(out=g_raw[:, 2 * q:2 * q + 2, :], in_=gv[:, 2 * q:2 * q + 2, :])
         p_raw = []
         for n in range(RT // 2):
-            host = 2 * n if 2 * n in P_TILES else 2 * n + 1
-            r = big.tile([P, 2, CONTR], BF16, name="p_raw%d" % n, offset=e32_offset(host))
+            r = big.tile([P, 2, CONTR], BF16, name="p_raw%d" % n, offset=e32_offset(2 * n))
             nc.sync.dma_start(out=r[:], in_=pv[:, 2 * n:2 * n + 2, :])
             p_raw.append(r)
 
@@ -262,13 +259,14 @@ def tile_differentiablematcher_t_kernel(tc, pred_masks, gt_masks, out):
                     out=acc[:, hs], in0=e32[NP + v][:, hs], scalar=a_all[:, NP + v:NP + v + 1],
                     in1=acc[:, hs], op0=ALU.mult, op1=ALU.add)
 
-        def col_pe(jc, g, width):
+        def col_pe(jc, g):
             k = 0
-            for c in range(g * GT, (g + 1) * GT):
+            lo, hi = P_PARTS[g]
+            for c in range(lo, hi):
                 for ea in (ehi[c], elo[c]):
-                    nc.tensor.matmul(csp_of[jc // 4][:, jc % 4, g, 0:width],
-                                     lhsT=ea[:, jc * P:(jc + 1) * P], rhs=mva[:, c, 0:width],
-                                     start=(k == 0), stop=(k == 2 * GT - 1))
+                    nc.tensor.matmul(csp_of[jc // 4][:, jc % 4, g, :],
+                                     lhsT=ea[:, jc * P:(jc + 1) * P], rhs=mva[:, c, :],
+                                     start=(k == 0), stop=(k == 2 * (hi - lo) - 1))
                     k += 1
 
         for s in range(-3, RT + 2):
@@ -290,8 +288,7 @@ def tile_differentiablematcher_t_kernel(tc, pred_masks, gt_masks, out):
             if 0 <= s + 3 < RT:
                 do_transposes(s + 3)
             if s in FIRST_A:
-                lo = FIRST_A[s] * GT
-                hi = lo + GT
+                lo, hi = P_PARTS[FIRST_A[s]]
                 nc.vector.tensor_reduce(out=s_all[:, lo:hi], in_=rs[:, lo:hi, :], axis=AX.X, op=ALU.add)
                 inverse_and_high(a_all[:, lo:hi], mva[:, lo:hi, :], s_all[:, lo:hi])
                 low_half(a_all[:, lo:hi], mva[:, lo:hi, :])
@@ -313,37 +310,21 @@ def tile_differentiablematcher_t_kernel(tc, pred_masks, gt_masks, out):
                 acc_step(v_late, 1)
             if back is not None:
                 for part in range(2):
-                    do_eb_copy(back, part, part == 1 or back % 2 == 0)
+                    do_eb_copy(back, part, part == 1 or back % 3 != 0)
             for jc in FIRST_COL.get(s, []):
                 if jc == 0:
                     csp = bank(1, [P, 2, 4, 2, 2], F32, "csp")
                     csp_of[0] = csp[:, 0]
                     csp_of[1] = csp[:, 1]
-                col_pe(jc, 0, 2)
+                col_pe(jc, 0)
 
         junk = big.tile([P, 512], F32, name="junk", offset=OFF_JUNK)
         sjunk = big.tile([P, 512], BF16, name="sjunk", offset=OFF_SJUNK)
         bcs = big.tile([P, COLS], F32, name="bcs", offset=OFF_BCS)
-        dm = bank(7, [P, 512], F32, "dm")
         bc = {}
         at_of = {}
         rsp = {}
         prod_of = {}
-        done = {"n": 0}
-
-        def wide_passes(n, width):
-            done["n"] = 0
-            for k in range(n):
-                nc.tensor.matmul_mx(
-                    out=dm[:, 0:width],
-                    lhsT=gc[(0, 0)][:, 0:P].bitcast(FP8X4), lhsT_scale=gs[(0, 0)][:, 0:P],
-                    rhs=gc[(0, 0)][:, 0:width].bitcast(FP8X4), rhs_scale=gs[(0, 0)][:, 0:width],
-                    start=True, stop=True)
-
-        def tick(n):
-            done["n"] += n
-            if done["n"] >= TICK:
-                wide_passes(1, 256)
 
         def broadcast(h):
             bc[h] = bank(2 + h, [P, 512], F32, "bc")
@@ -354,18 +335,17 @@ def tile_differentiablematcher_t_kernel(tc, pred_masks, gt_masks, out):
 
         def rows_pe(h, lo, hi):
             for c in range(lo, hi):
+                g = 0 if c < P_PARTS[1][0] else 1
                 k = 0
                 for jc in range(4 * h, 4 * h + 4):
                     for eb in (ebh[c], ebl[c]):
-                        nc.tensor.matmul(rsp[c // GT][:, c % GT, h, :], lhsT=eb[:, jc, :],
+                        nc.tensor.matmul(rsp[g][:, c - P_PARTS[g][0], h, :], lhsT=eb[:, jc, :],
                                          rhs=mvb[:, jc, :], start=(k == 0), stop=(k == 7))
                         k += 1
-                tick(8)
 
         def cols_pe(g, h):
             for jc in range(4 * h, 4 * h + 4):
-                col_pe(jc, g, NCOL)
-                tick(2 * GT)
+                col_pe(jc, g)
 
         def acc_turn(h):
             at_of[h] = bank(6, [P, 4, P], F32, "at")
@@ -395,7 +375,7 @@ def tile_differentiablematcher_t_kernel(tc, pred_masks, gt_masks, out):
         def b_steps(h, last):
             js = slice(4 * h, 4 * h + 4)
             sums = [
-                lambda: nc.vector.tensor_reduce(out=tt[:, js], in_=csp_of[h][:, :, :, 0:2],
+                lambda: nc.vector.tensor_reduce(out=tt[:, js], in_=csp_of[h][:, :, :, :],
                                                 axis=AX.XY, op=ALU.add),
                 lambda: nc.vector.tensor_tensor(out=tt[:, js], in0=tt[:, js], in1=acs[:, js], op=ALU.add),
             ]
@@ -407,9 +387,9 @@ def tile_differentiablematcher_t_kernel(tc, pred_masks, gt_masks, out):
             ]
 
         def p_steps(g):
-            cs = slice(g * GT, (g + 1) * GT)
+            cs = slice(P_PARTS[g][0], P_PARTS[g][1])
             return [
-                lambda: nc.vector.tensor_reduce(out=s_all[:, cs], in_=rsp[g][:, :, :, 0:2],
+                lambda: nc.vector.tensor_reduce(out=s_all[:, cs], in_=rsp[g][:],
                                                 axis=AX.XY, op=ALU.add),
                 lambda: inverse_and_high(a_all[:, cs], mva[:, cs, :], s_all[:, cs]),
                 lambda: low_half(a_all[:, cs], mva[:, cs, :]),
@@ -429,7 +409,7 @@ def tile_differentiablematcher_t_kernel(tc, pred_masks, gt_masks, out):
             nc.scalar.activation(out=r32[c][:], in_=r32[c][:], func=ACT.Copy, scale=a_all[:, c:c + 1])
 
         for jc in range(CC):
-            col_pe(jc, 1, 2)
+            col_pe(jc, 1)
         acc_turn(0)
         for i in range(2):
             for part in range(2):
@@ -444,28 +424,27 @@ def tile_differentiablematcher_t_kernel(tc, pred_masks, gt_masks, out):
         for it in range(1, ITERS):
             last = it == ITERS - 1
             broadcast(0)
-            wide_passes(4, 512)
             for g in range(2):
-                rsp[g] = bank(4 + g, [P, GT, 2, NCOL], F32, "rsp")
-            rows_pe(0, 0, 9)
+                rsp[g] = bank(4 + g, [P, P_PARTS[g][1] - P_PARTS[g][0], 2, NCOL], F32, "rsp")
+            rows_pe(0, 0, 4)
             acc_turn(1)
-            b1 = dict(zip((2, 3, 4, 5), b_steps(1, False)))
+            b1 = dict(zip((4, 5, 6, 7), b_steps(1, False)))
             for v in range(VR):
                 row_v(v, 0)
                 if v in b1:
                     b1[v]()
-            rows_pe(0, 9, 20)
+            rows_pe(0, 4, 15)
             for v in range(VR, NV):
                 row_g(v, 0)
                 row_gsum(v, 0)
-                if v == VR + 1:
+                if v == NV - 2:
                     broadcast(1)
-            rows_pe(0, 20, NP)
+            rows_pe(0, 15, NP)
             for v in range(VR, NV):
                 row_g(v, 1)
                 row_gsum(v, 1)
             rows_pe(1, 0, NP)
-            first = dict(zip((4, 5), v_steps(0, 4)))
+            first = dict(zip((6, 7), v_steps(0, 6)))
             for v in range(VR):
                 row_v(v, 1)
                 if v in first:
@@ -475,18 +454,18 @@ def tile_differentiablematcher_t_kernel(tc, pred_masks, gt_masks, out):
                     r32[c] = big.tile([P, COLS], F32, name="r32_%d" % c, offset=OFF_EB + c * 4 * KB)
                     if c < NP - REBUILT:
                         nc.sync.dma_start(out=r32[c][:], in_=ov[:, P_TILES[c], :])
-            extra = {}
-            for v, f in zip((0, 1, 2), p_steps(0)):
-                extra[v] = [f]
-            for v, f in zip((1, 2), v_steps(4, VR)):
+            extra = {v: [] for v in range(NV)}
+            for v, f in zip((1, 2, 3), p_steps(0)):
                 extra[v] = extra[v] + [f]
-            for v, f in zip((3, 4), v_steps(VR, NV)):
-                extra[v] = [f]
-            for v, f in zip((5, 6, 7), p_steps(1)):
-                extra[v] = [f]
+            for v, f in zip((2, 3), v_steps(6, VR)):
+                extra[v] = extra[v] + [f]
+            for v, f in zip((5, 6), v_steps(VR, NV)):
+                extra[v] = extra[v] + [f]
+            for v, f in zip((7, 8, 9), p_steps(1)):
+                extra[v] = extra[v] + [f]
             for v in range(NV):
                 acc_step(v, 0)
-                for f in extra.get(v, []):
+                for f in extra[v]:
                     f()
             for h in range(2):
                 csp_of[h] = bank(h, [P, 4, 2, NCOL], F32, "csp")
@@ -495,7 +474,7 @@ def tile_differentiablematcher_t_kernel(tc, pred_masks, gt_masks, out):
             cols_pe(1, 0)
             acc_turn(0)
             cols_pe(1, 1)
-            b0 = dict(zip((4, 5, 6, 7), b_steps(0, last)))
+            b0 = dict(zip((8, 9, 10, 11), b_steps(0, last)))
             for v in range(NV):
                 acc_step(v, 1)
                 if v in b0:
@@ -524,16 +503,23 @@ def tile_differentiablematcher_t_kernel(tc, pred_masks, gt_masks, out):
         for c in range(2):
             out_g(c, slice(0, 512))
         broadcast(1)
+        sum_banks = [(4, 5), (6, 7), (0, 1)]
         esum = {}
-        for h in range(2):
-            hs = slice(h * 512, (h + 1) * 512)
-            c = NP - 1
-            esum[h] = bank(4 + h, [P, 512], F32, "esum")
-            nc.tensor.matmul(esum[h][:], lhsT=ident_b[:], rhs=ehi[c][:, hs], start=True, stop=False)
-            nc.tensor.matmul(esum[h][:], lhsT=ident_b[:], rhs=elo[c][:, hs], start=False, stop=True)
-        for c in range(3, G_OUT):
+
+        def rebuild(i):
+            c = NP - REBUILT + i
+            for h in range(2):
+                hs = slice(h * 512, (h + 1) * 512)
+                e = bank(sum_banks[i % 3][h], [P, 512], F32, "esum")
+                nc.tensor.matmul(e[:], lhsT=ident_b[:], rhs=ehi[c][:, hs], start=True, stop=False)
+                nc.tensor.matmul(e[:], lhsT=ident_b[:], rhs=elo[c][:, hs], start=False, stop=True)
+                esum[(c, h)] = e
+
+        for i in range(3):
+            rebuild(i)
+        for c in range(3, NP - REBUILT):
             scale_rows(c)
-        for c in range(G_OUT):
+        for c in range(NP - REBUILT):
             out_g(c, slice(512, COLS) if c < 2 else slice(0, COLS))
             nc.scalar.dma_start(out=ov[:, P_TILES[c], :], in_=r32[c][:])
         for v in range(NV):
@@ -541,11 +527,13 @@ def tile_differentiablematcher_t_kernel(tc, pred_masks, gt_masks, out):
                 out_v(v, 0)
             out_v(v, 1)
             nc.sync.dma_start(out=ov[:, V_TILES[v], :], in_=e32[NP + v][:])
-        for c in [NP - 1] + list(range(G_OUT, NP - 1)):
+        for i in range(REBUILT):
+            c = NP - REBUILT + i
             for h in range(2):
                 hs = slice(h * 512, (h + 1) * 512)
                 nc.vector.scalar_tensor_tensor(
-                    out=r32[c][:, hs], in0=esum[h][:] if c == NP - 1 else r32[c][:, hs],
-                    scalar=a_all[:, c:c + 1], in1=bcs[:, hs] if c == NP - 1 else bc[h][:],
-                    op0=ALU.mult, op1=ALU.mult)
+                    out=r32[c][:, hs], in0=esum[(c, h)][:], scalar=a_all[:, c:c + 1],
+                    in1=bcs[:, hs], op0=ALU.mult, op1=ALU.mult)
+            if i + 3 < REBUILT:
+                rebuild(i + 3)
             nc.sync.dma_start(out=ov[:, P_TILES[c], :], in_=r32[c][:])

@@ -23,16 +23,18 @@ INV_TEMP = 10.0
 KB = 1024
 FLOPS = 2 * ROWS * COLS * CONTR
 
-NV = 13
+NV = 11
 NP = RT - NV
-V_TILES = [t for t in range(RT) if (NV * t + 20) % RT < NV]
+V_TILES = [t for t in range(RT) if (NV * t + 16) % RT < NV]
 P_TILES = [t for t in range(RT) if t not in V_TILES]
-P_PARTS = [(0, 10), (10, NP)]
+P_PARTS = [(0, 11), (11, NP)]
+FIRST_PARTS = [(0, 11), (11, 17), (17, NP)]
+FIRST_A = {20: 0, 29: 1, 32: 2}
+FIRST_COL = {21: [(0, 0)], 22: [(0, 1)], 23: [(0, 2)], 24: [(0, 3)], 25: [(0, 4)], 26: [(0, 5)],
+             27: [(0, 6)], 28: [(0, 7)], 30: [(1, 0), (1, 1)], 31: [(1, 2), (1, 3)],
+             32: [(1, 4), (1, 5)], 33: [(1, 6), (1, 7)]}
 NCOL = 2
 REBUILT = 8
-VR = 8
-FIRST_A = {20: 0, 32: 1}
-FIRST_COL = {21: [0], 22: [1], 23: [2], 24: [3], 25: [4], 26: [5], 27: [6], 28: [7]}
 
 OFF_EAH = 0
 OFF_EAL = OFF_EAH + NP * 2 * KB
@@ -259,9 +261,9 @@ def tile_differentiablematcher_t_kernel(tc, pred_masks, gt_masks, out):
                     out=acc[:, hs], in0=e32[NP + v][:, hs], scalar=a_all[:, NP + v:NP + v + 1],
                     in1=acc[:, hs], op0=ALU.mult, op1=ALU.add)
 
-        def col_pe(jc, g):
+        def col_pe(jc, g, parts):
             k = 0
-            lo, hi = P_PARTS[g]
+            lo, hi = parts[g]
             for c in range(lo, hi):
                 for ea in (ehi[c], elo[c]):
                     nc.tensor.matmul(csp_of[jc // 4][:, jc % 4, g, :],
@@ -288,7 +290,7 @@ def tile_differentiablematcher_t_kernel(tc, pred_masks, gt_masks, out):
             if 0 <= s + 3 < RT:
                 do_transposes(s + 3)
             if s in FIRST_A:
-                lo, hi = P_PARTS[FIRST_A[s]]
+                lo, hi = FIRST_PARTS[FIRST_A[s]]
                 nc.vector.tensor_reduce(out=s_all[:, lo:hi], in_=rs[:, lo:hi, :], axis=AX.X, op=ALU.add)
                 inverse_and_high(a_all[:, lo:hi], mva[:, lo:hi, :], s_all[:, lo:hi])
                 low_half(a_all[:, lo:hi], mva[:, lo:hi, :])
@@ -310,13 +312,13 @@ def tile_differentiablematcher_t_kernel(tc, pred_masks, gt_masks, out):
                 acc_step(v_late, 1)
             if back is not None:
                 for part in range(2):
-                    do_eb_copy(back, part, part == 1 or back % 3 != 0)
-            for jc in FIRST_COL.get(s, []):
-                if jc == 0:
-                    csp = bank(1, [P, 2, 4, 2, 2], F32, "csp")
+                    do_eb_copy(back, part, part == 1 or back % 2 == 0)
+            for g, jc in FIRST_COL.get(s, []):
+                if not csp_of:
+                    csp = bank(1, [P, 2, 4, len(FIRST_PARTS), NCOL], F32, "csp")
                     csp_of[0] = csp[:, 0]
                     csp_of[1] = csp[:, 1]
-                col_pe(jc, 0)
+                col_pe(jc, g, FIRST_PARTS)
 
         junk = big.tile([P, 512], F32, name="junk", offset=OFF_JUNK)
         sjunk = big.tile([P, 512], BF16, name="sjunk", offset=OFF_SJUNK)
@@ -324,13 +326,14 @@ def tile_differentiablematcher_t_kernel(tc, pred_masks, gt_masks, out):
         bc = {}
         at_of = {}
         rsp = {}
-        prod_of = {}
 
         def broadcast(h):
             bc[h] = bank(2 + h, [P, 512], F32, "bc")
             for jc in range(4 * h, 4 * h + 4):
                 o = bc[h][:, (jc % 4) * P:(jc % 4 + 1) * P]
                 nc.tensor.transpose(o, bv[:, jc:jc + 1].to_broadcast([P, P]), ident_f[:])
+
+        def spread(h):
             nc.scalar.copy(out=bcs[:, h * 512:(h + 1) * 512], in_=bc[h][:])
 
         def rows_pe(h, lo, hi):
@@ -343,9 +346,9 @@ def tile_differentiablematcher_t_kernel(tc, pred_masks, gt_masks, out):
                                          rhs=mvb[:, jc, :], start=(k == 0), stop=(k == 7))
                         k += 1
 
-        def cols_pe(g, h):
-            for jc in range(4 * h, 4 * h + 4):
-                col_pe(jc, g)
+        def cols_pe(g, lo, hi):
+            for jc in range(lo, hi):
+                col_pe(jc, g, P_PARTS)
 
         def acc_turn(h):
             at_of[h] = bank(6, [P, 4, P], F32, "at")
@@ -361,16 +364,6 @@ def tile_differentiablematcher_t_kernel(tc, pred_masks, gt_masks, out):
             nc.vector.scalar_tensor_tensor(
                 out=junk[:], in0=e32[NP + v][:, h * 512:(h + 1) * 512], scalar=1.0,
                 in1=bc[h][:], op0=ALU.mult, op1=ALU.mult, accum_out=svh[:, v, h:h + 1])
-
-        def row_g(v, h):
-            pr = big.tile([P, 512], F32, name="prod%d" % (v % 2), offset=OFF_GRP + (v % 2) * 2 * KB)
-            hs = slice(h * 512, (h + 1) * 512)
-            nc.gpsimd.tensor_tensor(out=pr[:], in0=e32[NP + v][:, hs], in1=bcs[:, hs], op=ALU.mult)
-            prod_of[(v, h)] = pr
-
-        def row_gsum(v, h):
-            nc.scalar.activation(out=sjunk[:], in_=prod_of[(v, h)][:], func=ACT.Copy,
-                                 accum_out=svh[:, v, h:h + 1])
 
         def b_steps(h, last):
             js = slice(4 * h, 4 * h + 4)
@@ -409,9 +402,9 @@ def tile_differentiablematcher_t_kernel(tc, pred_masks, gt_masks, out):
             nc.scalar.activation(out=r32[c][:], in_=r32[c][:], func=ACT.Copy, scale=a_all[:, c:c + 1])
 
         for jc in range(CC):
-            col_pe(jc, 1)
-        acc_turn(0)
+            col_pe(jc, 2, FIRST_PARTS)
         for i in range(2):
+            acc_turn(i)
             for part in range(2):
                 do_eb_transposes(NP - 2 + i, part, 2 + 2 * i + part)
         for i in range(2):
@@ -426,26 +419,17 @@ def tile_differentiablematcher_t_kernel(tc, pred_masks, gt_masks, out):
             broadcast(0)
             for g in range(2):
                 rsp[g] = bank(4 + g, [P, P_PARTS[g][1] - P_PARTS[g][0], 2, NCOL], F32, "rsp")
-            rows_pe(0, 0, 4)
-            acc_turn(1)
-            b1 = dict(zip((4, 5, 6, 7), b_steps(1, False)))
-            for v in range(VR):
+            rows_pe(0, 0, 8)
+            b1 = dict(zip((0, 1, 2, 3), b_steps(1, False)))
+            for v in range(NV):
                 row_v(v, 0)
                 if v in b1:
                     b1[v]()
-            rows_pe(0, 4, 15)
-            for v in range(VR, NV):
-                row_g(v, 0)
-                row_gsum(v, 0)
-                if v == NV - 2:
-                    broadcast(1)
-            rows_pe(0, 15, NP)
-            for v in range(VR, NV):
-                row_g(v, 1)
-                row_gsum(v, 1)
+            broadcast(1)
+            rows_pe(0, 8, NP)
             rows_pe(1, 0, NP)
-            first = dict(zip((6, 7), v_steps(0, 6)))
-            for v in range(VR):
+            first = dict(zip((8, 9), v_steps(0, 8)))
+            for v in range(NV):
                 row_v(v, 1)
                 if v in first:
                     first[v]()
@@ -455,13 +439,11 @@ def tile_differentiablematcher_t_kernel(tc, pred_masks, gt_masks, out):
                     if c < NP - REBUILT:
                         nc.sync.dma_start(out=r32[c][:], in_=ov[:, P_TILES[c], :])
             extra = {v: [] for v in range(NV)}
-            for v, f in zip((1, 2, 3), p_steps(0)):
+            for v, f in zip((0, 1, 2), p_steps(0)):
                 extra[v] = extra[v] + [f]
-            for v, f in zip((2, 3), v_steps(6, VR)):
+            for v, f in zip((0, 1), v_steps(8, NV)):
                 extra[v] = extra[v] + [f]
-            for v, f in zip((5, 6), v_steps(VR, NV)):
-                extra[v] = extra[v] + [f]
-            for v, f in zip((7, 8, 9), p_steps(1)):
+            for v, f in zip((5, 6, 7), p_steps(1)):
                 extra[v] = extra[v] + [f]
             for v in range(NV):
                 acc_step(v, 0)
@@ -469,19 +451,22 @@ def tile_differentiablematcher_t_kernel(tc, pred_masks, gt_masks, out):
                     f()
             for h in range(2):
                 csp_of[h] = bank(h, [P, 4, 2, NCOL], F32, "csp")
-            cols_pe(0, 0)
-            cols_pe(0, 1)
-            cols_pe(1, 0)
+            cols_pe(0, 0, CC)
             acc_turn(0)
-            cols_pe(1, 1)
-            b0 = dict(zip((8, 9, 10, 11), b_steps(0, last)))
-            for v in range(NV):
-                acc_step(v, 1)
-                if v in b0:
-                    b0[v]()
             if last:
                 for c in range(3):
                     scale_rows(c)
+            cols_pe(1, 0, 4)
+            b0 = b_steps(0, last)
+            for v in range(NV):
+                acc_step(v, 1)
+                if v == NV - 2:
+                    b0[0]()
+            cols_pe(1, 4, 6)
+            acc_turn(1)
+            cols_pe(1, 6, CC)
+            for f in b0[1:]:
+                f()
 
         def out_v(v, h):
             hs = slice(h * 512, (h + 1) * 512)
@@ -494,15 +479,17 @@ def tile_differentiablematcher_t_kernel(tc, pred_masks, gt_masks, out):
                                     op=ALU.mult)
 
         broadcast(0)
-        acc_turn(1)
+        spread(0)
         b1 = b_steps(1, True)
         for v in range(4):
             out_v(v, 0)
-            if v >= 1:
-                b1[v - 1]()
+            nc.sync.dma_start(out=ov[:, V_TILES[v], 0:512], in_=e32[NP + v][:, 0:512])
+            if v < 3:
+                b1[v]()
         for c in range(2):
             out_g(c, slice(0, 512))
         broadcast(1)
+        spread(1)
         sum_banks = [(4, 5), (6, 7), (0, 1)]
         esum = {}
 
@@ -523,10 +510,11 @@ def tile_differentiablematcher_t_kernel(tc, pred_masks, gt_masks, out):
             out_g(c, slice(512, COLS) if c < 2 else slice(0, COLS))
             nc.scalar.dma_start(out=ov[:, P_TILES[c], :], in_=r32[c][:])
         for v in range(NV):
+            cols = slice(512, COLS) if v < 4 else slice(0, COLS)
             if v >= 4:
                 out_v(v, 0)
             out_v(v, 1)
-            nc.sync.dma_start(out=ov[:, V_TILES[v], :], in_=e32[NP + v][:])
+            nc.sync.dma_start(out=ov[:, V_TILES[v], cols], in_=e32[NP + v][:, cols])
         for i in range(REBUILT):
             c = NP - REBUILT + i
             for h in range(2):

@@ -29,9 +29,9 @@ V_TILES = [t for t in range(RT) if (NV * t + 16) % RT < NV]
 P_TILES = [t for t in range(RT) if t not in V_TILES]
 P_PARTS = [(0, 11), (11, NP)]
 FIRST_PARTS = [(0, 11), (11, 17), (17, NP)]
-FIRST_A = {20: 0, 29: 1, 32: 2}
-FIRST_COL = {21: [(0, 0)], 22: [(0, 1)], 23: [(0, 2)], 24: [(0, 3)], 25: [(0, 4)], 26: [(0, 5)],
-             27: [(0, 6)], 28: [(0, 7)], 30: [(1, 0), (1, 1)], 31: [(1, 2), (1, 3)],
+FIRST_A = {19: 0, 29: 1, 32: 2}
+FIRST_COL = {20: [(0, 0)], 21: [(0, 1)], 22: [(0, 2)], 23: [(0, 3)], 24: [(0, 4)], 25: [(0, 5)],
+             26: [(0, 6)], 27: [(0, 7)], 30: [(1, 0), (1, 1)], 31: [(1, 2), (1, 3)],
              32: [(1, 4), (1, 5)], 33: [(1, 6), (1, 7)]}
 NCOL = 2
 REBUILT = 8
@@ -242,10 +242,13 @@ def tile_differentiablematcher_t_kernel(tc, pred_masks, gt_masks, out):
         acc = big.tile([P, COLS], F32, name="acc", offset=OFF_ACC)
         csp_of = {}
 
-        def inverse_and_high(vec, mv, sums):
+        def inverse_and_high(vec, mv, sums, on_vector):
             nc.vector.reciprocal(out=vec, in_=sums)
-            with nc.allow_low_precision(reason="the high half; the low half follows"):
-                nc.vector.reciprocal(out=mv[:, :, 0:1], in_=sums.unsqueeze(2))
+            if on_vector:
+                with nc.allow_low_precision(reason="the high half; the low half follows"):
+                    nc.vector.reciprocal(out=mv[:, :, 0:1], in_=sums.unsqueeze(2))
+            else:
+                nc.scalar.copy(out=mv[:, :, 0:1], in_=vec.unsqueeze(2))
 
         def low_half(vec, mv):
             nc.vector.tensor_tensor(out=mv[:, :, 1:2], in0=vec.unsqueeze(2), in1=mv[:, :, 0:1],
@@ -292,7 +295,7 @@ def tile_differentiablematcher_t_kernel(tc, pred_masks, gt_masks, out):
             if s in FIRST_A:
                 lo, hi = FIRST_PARTS[FIRST_A[s]]
                 nc.vector.tensor_reduce(out=s_all[:, lo:hi], in_=rs[:, lo:hi, :], axis=AX.X, op=ALU.add)
-                inverse_and_high(a_all[:, lo:hi], mva[:, lo:hi, :], s_all[:, lo:hi])
+                inverse_and_high(a_all[:, lo:hi], mva[:, lo:hi, :], s_all[:, lo:hi], True)
                 low_half(a_all[:, lo:hi], mva[:, lo:hi, :])
             c = None if v_late is None else slice(NP + v_late, NP + v_late + 1)
             if c is not None:
@@ -320,12 +323,12 @@ def tile_differentiablematcher_t_kernel(tc, pred_masks, gt_masks, out):
                     csp_of[1] = csp[:, 1]
                 col_pe(jc, g, FIRST_PARTS)
 
-        junk = big.tile([P, 512], F32, name="junk", offset=OFF_JUNK)
         sjunk = big.tile([P, 512], BF16, name="sjunk", offset=OFF_SJUNK)
         bcs = big.tile([P, COLS], F32, name="bcs", offset=OFF_BCS)
         bc = {}
         at_of = {}
         rsp = {}
+        junk = big.tile([P, 512], F32, name="junk", offset=OFF_JUNK)
 
         def broadcast(h):
             bc[h] = bank(2 + h, [P, 512], F32, "bc")
@@ -351,7 +354,7 @@ def tile_differentiablematcher_t_kernel(tc, pred_masks, gt_masks, out):
                 col_pe(jc, g, P_PARTS)
 
         def acc_turn(h):
-            at_of[h] = bank(6, [P, 4, P], F32, "at")
+            at_of[h] = bank(6 + h, [P, 4, P], F32, "at")
             for j in range(4):
                 jc = 4 * h + j
                 nc.tensor.transpose(at_of[h][:, j, :], acc[:, jc * P:(jc + 1) * P], ident_f[:])
@@ -361,9 +364,17 @@ def tile_differentiablematcher_t_kernel(tc, pred_masks, gt_masks, out):
                                      accum_out=acs[:, jc:jc + 1])
 
         def row_v(v, h):
-            nc.vector.scalar_tensor_tensor(
-                out=junk[:], in0=e32[NP + v][:, h * 512:(h + 1) * 512], scalar=1.0,
-                in1=bc[h][:], op0=ALU.mult, op1=ALU.mult, accum_out=svh[:, v, h:h + 1])
+            hs = slice(h * 512, (h + 1) * 512)
+            if v % 2 == 0:
+                nc.vector.scalar_tensor_tensor(
+                    out=junk[:], in0=e32[NP + v][:, hs], scalar=1.0, in1=bc[h][:],
+                    op0=ALU.mult, op1=ALU.mult, accum_out=svh[:, v, h:h + 1])
+            else:
+                i = v // 2 % 2
+                pr = big.tile([P, 512], F32, name="prod%d" % i, offset=OFF_GRP + i * 2 * KB)
+                nc.vector.tensor_tensor(out=pr[:], in0=e32[NP + v][:, hs], in1=bc[h][:], op=ALU.mult)
+                nc.scalar.activation(out=sjunk[:], in_=pr[:], func=ACT.Copy,
+                                     accum_out=svh[:, v, h:h + 1])
 
         def b_steps(h, last):
             js = slice(4 * h, 4 * h + 4)
@@ -375,7 +386,7 @@ def tile_differentiablematcher_t_kernel(tc, pred_masks, gt_masks, out):
             if last:
                 return sums + [lambda: nc.vector.reciprocal(out=bv[:, js], in_=tt[:, js])]
             return sums + [
-                lambda: inverse_and_high(bv[:, js], mvb[:, js, :], tt[:, js]),
+                lambda: inverse_and_high(bv[:, js], mvb[:, js, :], tt[:, js], False),
                 lambda: low_half(bv[:, js], mvb[:, js, :]),
             ]
 
@@ -384,7 +395,7 @@ def tile_differentiablematcher_t_kernel(tc, pred_masks, gt_masks, out):
             return [
                 lambda: nc.vector.tensor_reduce(out=s_all[:, cs], in_=rsp[g][:],
                                                 axis=AX.XY, op=ALU.add),
-                lambda: inverse_and_high(a_all[:, cs], mva[:, cs, :], s_all[:, cs]),
+                lambda: inverse_and_high(a_all[:, cs], mva[:, cs, :], s_all[:, cs], False),
                 lambda: low_half(a_all[:, cs], mva[:, cs, :]),
             ]
 
@@ -407,11 +418,10 @@ def tile_differentiablematcher_t_kernel(tc, pred_masks, gt_masks, out):
             acc_turn(i)
             for part in range(2):
                 do_eb_transposes(NP - 2 + i, part, 2 + 2 * i + part)
-        for i in range(2):
-            do_eb_copy(NP - 2 + i, 0, False)
         for f in b_steps(0, False):
             f()
         for i in range(2):
+            do_eb_copy(NP - 2 + i, 0, False)
             do_eb_copy(NP - 2 + i, 1, True)
 
         for it in range(1, ITERS):
@@ -419,50 +429,46 @@ def tile_differentiablematcher_t_kernel(tc, pred_masks, gt_masks, out):
             broadcast(0)
             for g in range(2):
                 rsp[g] = bank(4 + g, [P, P_PARTS[g][1] - P_PARTS[g][0], 2, NCOL], F32, "rsp")
-            rows_pe(0, 0, 8)
-            b1 = dict(zip((0, 1, 2, 3), b_steps(1, False)))
+            rows_pe(0, 0, 12)
+            b1 = dict(zip((1, 2, 3, 5), b_steps(1, False)))
             for v in range(NV):
                 row_v(v, 0)
                 if v in b1:
                     b1[v]()
             broadcast(1)
-            rows_pe(0, 8, NP)
+            rows_pe(0, 12, NP)
             rows_pe(1, 0, NP)
-            first = dict(zip((8, 9), v_steps(0, 8)))
+            p0 = p_steps(0)
+            v0 = v_steps(0, 7)
             for v in range(NV):
                 row_v(v, 1)
-                if v in first:
-                    first[v]()
+                if v == NV - 2:
+                    p0[0]()
+            for step in (v0[0], p0[1], v0[1], p0[2]):
+                step()
             if last:
                 for c in range(NP):
                     r32[c] = big.tile([P, COLS], F32, name="r32_%d" % c, offset=OFF_EB + c * 4 * KB)
                     if c < NP - REBUILT:
                         nc.sync.dma_start(out=r32[c][:], in_=ov[:, P_TILES[c], :])
-            extra = {v: [] for v in range(NV)}
-            for v, f in zip((0, 1, 2), p_steps(0)):
-                extra[v] = extra[v] + [f]
-            for v, f in zip((0, 1), v_steps(8, NV)):
-                extra[v] = extra[v] + [f]
-            for v, f in zip((5, 6, 7), p_steps(1)):
-                extra[v] = extra[v] + [f]
-            for v in range(NV):
+            extra = dict(zip((1, 2, 3, 4, 5), v_steps(7, NV) + p_steps(1)))
+            for v in range(NV - 1):
                 acc_step(v, 0)
-                for f in extra[v]:
-                    f()
+                acc_step(v, 1)
+                if v in extra:
+                    extra[v]()
             for h in range(2):
                 csp_of[h] = bank(h, [P, 4, 2, NCOL], F32, "csp")
             cols_pe(0, 0, CC)
-            acc_turn(0)
             if last:
                 for c in range(3):
                     scale_rows(c)
-            cols_pe(1, 0, 4)
+            cols_pe(1, 0, 6)
             b0 = b_steps(0, last)
-            for v in range(NV):
-                acc_step(v, 1)
-                if v == NV - 2:
-                    b0[0]()
-            cols_pe(1, 4, 6)
+            b0[0]()
+            acc_step(NV - 1, 0)
+            acc_step(NV - 1, 1)
+            acc_turn(0)
             acc_turn(1)
             cols_pe(1, 6, CC)
             for f in b0[1:]:

from contextlib import ExitStack

import concourse.mybir as mybir
from concourse.masks import make_identity

F32 = mybir.dt.float32
BF16 = mybir.dt.bfloat16
U32 = mybir.dt.uint32
U8 = mybir.dt.uint8
FP8X4 = mybir.dt.float8_e4m3fn_x4
ALU = mybir.AluOpType
ACT = mybir.ActivationFunctionType
AX = mybir.AxisListType

P = 128
ROWS = 4096
COLS = 1024
CONTR = 1024
RT = ROWS // P
CC = COLS // P
ITERS = 5
INV_TEMP = 10.0
KB = 1024
FLOPS = 2 * ROWS * COLS * CONTR

NV = 11
NP = RT - NV
V_TILES = [t for t in range(RT) if (NV * t + 16) % RT < NV]
P_TILES = [t for t in range(RT) if t not in V_TILES]
P_PARTS = [(0, 11), (11, NP)]
FIRST_PARTS = [(0, 11), (11, 17), (17, NP)]
FIRST_A = {19: 0, 29: 1, 32: 2}
FIRST_COL = {20: [(0, 0)], 21: [(0, 1)], 22: [(0, 2)], 23: [(0, 3)], 24: [(0, 4)], 25: [(0, 5)],
             26: [(0, 6)], 27: [(0, 7)], 30: [(1, 0), (1, 1)], 31: [(1, 2), (1, 3)],
             32: [(1, 4), (1, 5)], 33: [(1, 6), (1, 7)]}
NCOL = 2
REBUILT = 8

OFF_EAH = 0
OFF_EAL = OFF_EAH + NP * 2 * KB
OFF_EB = OFF_EAL + NP * 2 * KB
OFF_EV = OFF_EB + NP * 4 * KB
OFF_MISC = OFF_EV + NV * 4 * KB
OFF_GRAW = OFF_EAH + (NP - 8) * 2 * KB
OFF_GGRP = OFF_EAL + (NP - 8) * 2 * KB
OFF_GC = OFF_MISC
OFF_GS = OFF_MISC + 8 * KB
OFF_JUNK = OFF_MISC + 2 * KB
OFF_BCS = OFF_MISC + 4 * KB
OFF_SJUNK = OFF_MISC + 8 * KB + 512
OFF_GRP = OFF_MISC + 10 * KB
OFF_COD = OFF_MISC + 14 * KB
OFF_PLN = OFF_MISC + 17 * KB
OFF_ACC = OFF_PLN + 3 * 256


def tile_differentiablematcher_t_kernel(tc, pred_masks, gt_masks, out):
    nc = tc.nc
    pv = pred_masks.rearrange("b (p t) h w -> (b p) t (h w)", t=RT)
    gv = gt_masks.rearrange("(c p) h w -> p c (h w)", p=P)
    ov = out.rearrange("b (p t) n -> (b p) t n", t=RT)

    with ExitStack() as ctx:
        big = ctx.enter_context(tc.tile_pool(name="big", bufs=1))
        small = ctx.enter_context(tc.tile_pool(name="small", bufs=1))
        tiny = ctx.enter_context(tc.tile_pool(name="tiny", bufs=2))
        ps = ctx.enter_context(tc.psum_pool(name="ps", bufs=1))
        ctx.enter_context(tc.manual_schedule())

        def bank(b, shape, dtype, name):
            return ps.tile(shape, dtype, name=name, tag="bk%d" % b)

        def col_of(t):
            return P_TILES.index(t) if t in P_TILES else NP + V_TILES.index(t)

        def e32_offset(t):
            if t in P_TILES:
                return OFF_EB + P_TILES.index(t) * 4 * KB
            return OFF_EV + V_TILES.index(t) * 4 * KB

        g_raw = big.tile([P, CC, CONTR], BF16, name="g_raw", offset=OFF_GRAW)
        for q in range(4):
            nc.sync.dma_start(out=g_raw[:, 2 * q:2 * q + 2, :], in_=gv[:, 2 * q:2 * q + 2, :])
        p_raw = []
        for n in range(RT // 2):
            r = big.tile([P, 2, CONTR], BF16, name="p_raw%d" % n, offset=e32_offset(2 * n))
            nc.sync.dma_start(out=r[:], in_=pv[:, 2 * n:2 * n + 2, :])
            p_raw.append(r)

        ident_f = small.tile([P, P], F32, name="ident_f")
        make_identity(nc, ident_f[:])
        ident_b = small.tile([P, P], BF16, name="ident_b")
        make_identity(nc, ident_b[:])
        mva = small.tile([P, NP, NCOL], BF16, name="mva")
        nc.vector.memset(mva[:], 0.0)
        mvb = small.tile([P, CC, NCOL], BF16, name="mvb")
        nc.vector.memset(mvb[:], 0.0)
        rs = small.tile([P, RT, 2], F32, name="rs")
        s_all = small.tile([P, RT], F32, name="s_all")
        a_all = small.tile([P, RT], F32, name="a_all")
        svh = small.tile([P, NV, 2], F32, name="svh")
        acs = small.tile([P, CC], F32, name="acs")
        tt = small.tile([P, CC], F32, name="tt")
        bv = small.tile([P, CC], F32, name="bv")

        g_grp = big.tile([P, 2, 4 * COLS], BF16, name="g_grp", offset=OFF_GGRP, align_bytes=64)
        g_grp_w = g_grp[:].bitcast(F32).rearrange("p g (j u) -> p g j u", u=2)
        gc = {}
        gs = {}
        for g in range(2):
            for half in range(2):
                q = 2 * g + half
                gc[(g, half)] = big.tile([P, 512], U32, name="gc%d" % q,
                                         offset=OFF_GC + q * 2 * KB, align_bytes=64)
                gs[(g, half)] = big.tile([P, 512], U8, name="gs%d" % q,
                                         offset=OFF_GS + q * 512, align_bytes=64)
        for half in range(2):
            for jc in range(4 * half, 4 * half + 4):
                tpg = bank(jc, [P, 2, 2, P], F32, "tpg")
                src = g_raw[:, jc, :].bitcast(F32)
                for g in range(2):
                    for u in range(2):
                        lo = 256 * g + u
                        nc.tensor.transpose(tpg[:, g, u, :], src[:, lo:lo + 255:2], ident_f[:])
                dst = g_grp_w[:, :, jc * P:(jc + 1) * P, :]
                if jc % 2 == 0:
                    nc.vector.tensor_copy(out=dst, in_=tpg[:].rearrange("p g u w -> p g w u"))
                else:
                    nc.scalar.copy(out=dst, in_=tpg[:].rearrange("p g u w -> p g w u"))
            for g in range(2):
                nc.vector.quantize_mx(
                    out=gc[(g, half)][:].bitcast(FP8X4),
                    scales=gs[(g, half)][:],
                    in_=g_grp[:, g, half * 2048:(half + 1) * 2048],
                )

        tp_of = {}
        grp_of = {}
        cod_of = {}
        d_of = {}
        m2_of = {}
        nb_of = {}
        e32 = {}
        ehi = {}
        elo = {}
        ebp_of = {}
        ebh = {}
        ebl = {}

        def do_transposes(t):
            src = p_raw[t // 2][:, t % 2, :].bitcast(F32)
            tp_of[t] = bank(0, [P, 2, 2, P], F32, "tp")
            for g in range(2):
                for u in range(2):
                    lo = 256 * g + u
                    nc.tensor.transpose(tp_of[t][:, g, u, :], src[:, lo:lo + 255:2], ident_f[:])

        def do_regroup(t):
            grp = big.tile([P, 4 * 256], BF16, name="grp%d" % (t % 2),
                           offset=OFF_GRP + (t % 2) * 2 * KB, align_bytes=64)
            nc.scalar.copy(out=grp[:].bitcast(F32).rearrange("p (g i u) -> p g i u", g=2, u=2),
                           in_=tp_of[t][:].rearrange("p g u i -> p g i u"))
            grp_of[t] = grp

        def do_quantise(t):
            cod = big.tile([P, 256], U32, name="cod%d" % (t % 3),
                           offset=OFF_COD + (t % 3) * KB, align_bytes=64)
            pln = big.tile([P, 256], U8, name="pln%d" % (t % 3),
                           offset=OFF_PLN + (t % 3) * 256, align_bytes=64)
            nc.vector.quantize_mx(out=cod[:].bitcast(FP8X4), scales=pln[:], in_=grp_of[t][:])
            cod_of[t] = (cod, pln)

        def do_mx(t, h):
            cod, pln = cod_of[t]
            d = bank(2 + 2 * (t % 2) + h, [P, 512], F32, "d")
            for g in range(2):
                nc.tensor.matmul_mx(
                    out=d[:],
                    lhsT=cod[:, g * P:(g + 1) * P].bitcast(FP8X4),
                    lhsT_scale=pln[:, g * P:(g + 1) * P],
                    rhs=gc[(g, h)][:].bitcast(FP8X4),
                    rhs_scale=gs[(g, h)][:],
                    start=(g == 0),
                    stop=(g == 1),
                )
            d_of[(t, h)] = d

        def do_max(t, h):
            if h == 0:
                m2_of[t] = tiny.tile([P, 2], F32, name="m2")
            nc.vector.tensor_reduce(out=m2_of[t][:, h:h + 1], in_=d_of[(t, h)][:], axis=AX.X, op=ALU.max)

        def do_bias(t):
            m2 = m2_of[t]
            nb = tiny.tile([P, 1], F32, name="nb")
            nc.vector.tensor_scalar(out=nb[:], in0=m2[:, 0:1], scalar1=m2[:, 1:2],
                                    scalar2=-INV_TEMP, op0=ALU.max, op1=ALU.mult)
            nb_of[t] = nb

        def do_exp(t):
            c = col_of(t)
            e32[c] = big.tile([P, COLS], F32, name="e32_%d" % c, offset=e32_offset(t))
            if c < NP:
                ehi[c] = big.tile([P, COLS], BF16, name="eah%d" % c, offset=OFF_EAH + c * 2 * KB)
            for h in range(2):
                hs = slice(h * 512, (h + 1) * 512)
                nc.scalar.activation(out=e32[c][:, hs], in_=d_of[(t, h)][:], func=ACT.Exp,
                                     bias=nb_of[t][:, 0:1], scale=INV_TEMP,
                                     accum_out=rs[:, c, h:h + 1])
                if c < NP:
                    nc.scalar.activation(out=ehi[c][:, hs], in_=d_of[(t, h)][:], func=ACT.Exp,
                                         bias=nb_of[t][:, 0:1], scale=INV_TEMP)
            if c < NP - REBUILT:
                nc.sync.dma_start(out=ov[:, t, :], in_=e32[c][:])

        def do_sub(c):
            elo[c] = big.tile([P, COLS], BF16, name="elo%d" % c, offset=OFF_EAL + c * 2 * KB)
            for h in range(2):
                hs = slice(h * 512, (h + 1) * 512)
                nc.gpsimd.tensor_tensor(out=elo[c][:, hs], in0=e32[c][:, hs], in1=ehi[c][:, hs],
                                        op=ALU.subtract)

        def do_eb_transposes(c, part, b):
            src = ehi[c] if part == 0 else elo[c]
            ebp = bank(b, [P, CC, P], BF16, "ebp")
            for jc in range(CC):
                nc.tensor.transpose(ebp[:, jc, :], src[:, jc * P:(jc + 1) * P], ident_b[:])
            ebp_of[(c, part)] = ebp

        def do_eb_copy(c, part, on_vector):
            eb = big.tile([P, CC, P], BF16, name="eb%d_%d" % (part, c),
                          offset=OFF_EB + c * 4 * KB + part * 2 * KB)
            if on_vector:
                nc.vector.tensor_copy(out=eb[:], in_=ebp_of[(c, part)][:])
            else:
                nc.scalar.copy(out=eb[:], in_=ebp_of[(c, part)][:])
            if part == 0:
                ebh[c] = eb
            else:
                ebl[c] = eb

        acc = big.tile([P, COLS], F32, name="acc", offset=OFF_ACC)
        csp_of = {}

        def inverse_and_high(vec, mv, sums, on_vector):
            nc.vector.reciprocal(out=vec, in_=sums)
            if on_vector:
                with nc.allow_low_precision(reason="the high half; the low half follows"):
                    nc.vector.reciprocal(out=mv[:, :, 0:1], in_=sums.unsqueeze(2))
            else:
                nc.scalar.copy(out=mv[:, :, 0:1], in_=vec.unsqueeze(2))

        def low_half(vec, mv):
            nc.vector.tensor_tensor(out=mv[:, :, 1:2], in0=vec.unsqueeze(2), in1=mv[:, :, 0:1],
                                    op=ALU.subtract)

        def acc_step(v, h):
            hs = slice(h * 512, (h + 1) * 512)
            if v == 0:
                nc.vector.tensor_scalar(out=acc[:, hs], in0=e32[NP + v][:, hs],
                                        scalar1=a_all[:, NP:NP + 1], scalar2=None, op0=ALU.mult)
            else:
                nc.vector.scalar_tensor_tensor(
                    out=acc[:, hs], in0=e32[NP + v][:, hs], scalar=a_all[:, NP + v:NP + v + 1],
                    in1=acc[:, hs], op0=ALU.mult, op1=ALU.add)

        def col_pe(jc, g, parts):
            k = 0
            lo, hi = parts[g]
            for c in range(lo, hi):
                for ea in (ehi[c], elo[c]):
                    nc.tensor.matmul(csp_of[jc // 4][:, jc % 4, g, :],
                                     lhsT=ea[:, jc * P:(jc + 1) * P], rhs=mva[:, c, :],
                                     start=(k == 0), stop=(k == 2 * (hi - lo) - 1))
                    k += 1

        for s in range(-3, RT + 2):
            late = s - 2
            v_late = V_TILES.index(late) if late in V_TILES else None
            back = P_TILES.index(s - 4) if s - 4 in P_TILES[:NP - 2] else None
            if 0 <= s + 2 < RT:
                do_regroup(s + 2)
            if 0 <= s - 1 < RT:
                do_exp(s - 1)
            if late in P_TILES:
                do_sub(P_TILES.index(late))
            for h in range(2):
                if 0 <= s < RT:
                    do_mx(s, h)
            if back is not None:
                for part in range(2):
                    do_eb_transposes(back, part, 6 + part)
            if 0 <= s + 3 < RT:
                do_transposes(s + 3)
            if s in FIRST_A:
                lo, hi = FIRST_PARTS[FIRST_A[s]]
                nc.vector.tensor_reduce(out=s_all[:, lo:hi], in_=rs[:, lo:hi, :], axis=AX.X, op=ALU.add)
                inverse_and_high(a_all[:, lo:hi], mva[:, lo:hi, :], s_all[:, lo:hi], True)
                low_half(a_all[:, lo:hi], mva[:, lo:hi, :])
            c = None if v_late is None else slice(NP + v_late, NP + v_late + 1)
            if c is not None:
                nc.vector.tensor_reduce(out=s_all[:, c], in_=rs[:, c, :], axis=AX.X, op=ALU.add)
            if 0 <= s < RT:
                do_max(s, 0)
            if c is not None:
                nc.vector.reciprocal(out=a_all[:, c], in_=s_all[:, c])
            if 0 <= s < RT:
                do_max(s, 1)
            if 0 <= s + 2 < RT:
                do_quantise(s + 2)
            if 0 <= s < RT:
                do_bias(s)
            if c is not None:
                acc_step(v_late, 0)
                acc_step(v_late, 1)
            if back is not None:
                for part in range(2):
                    do_eb_copy(back, part, part == 1 or back % 2 == 0)
            for g, jc in FIRST_COL.get(s, []):
                if not csp_of:
                    csp = bank(1, [P, 2, 4, len(FIRST_PARTS), NCOL], F32, "csp")
                    csp_of[0] = csp[:, 0]
                    csp_of[1] = csp[:, 1]
                col_pe(jc, g, FIRST_PARTS)

        sjunk = big.tile([P, 512], BF16, name="sjunk", offset=OFF_SJUNK)
        bcs = big.tile([P, COLS], F32, name="bcs", offset=OFF_BCS)
        bc = {}
        at_of = {}
        rsp = {}
        junk = big.tile([P, 512], F32, name="junk", offset=OFF_JUNK)

        def broadcast(h):
            bc[h] = bank(2 + h, [P, 512], F32, "bc")
            for jc in range(4 * h, 4 * h + 4):
                o = bc[h][:, (jc % 4) * P:(jc % 4 + 1) * P]
                nc.tensor.transpose(o, bv[:, jc:jc + 1].to_broadcast([P, P]), ident_f[:])

        def spread(h):
            nc.scalar.copy(out=bcs[:, h * 512:(h + 1) * 512], in_=bc[h][:])

        def rows_pe(h, lo, hi):
            for c in range(lo, hi):
                g = 0 if c < P_PARTS[1][0] else 1
                k = 0
                for jc in range(4 * h, 4 * h + 4):
                    for eb in (ebh[c], ebl[c]):
                        nc.tensor.matmul(rsp[g][:, c - P_PARTS[g][0], h, :], lhsT=eb[:, jc, :],
                                         rhs=mvb[:, jc, :], start=(k == 0), stop=(k == 7))
                        k += 1

        def cols_pe(g, lo, hi):
            for jc in range(lo, hi):
                col_pe(jc, g, P_PARTS)

        def acc_turn(h):
            at_of[h] = bank(6 + h, [P, 4, P], F32, "at")
            for j in range(4):
                jc = 4 * h + j
                nc.tensor.transpose(at_of[h][:, j, :], acc[:, jc * P:(jc + 1) * P], ident_f[:])
            for j in range(4):
                jc = 4 * h + j
                nc.scalar.activation(out=sjunk[:, 0:P], in_=at_of[h][:, j, :], func=ACT.Copy,
                                     accum_out=acs[:, jc:jc + 1])

        def row_v(v, h):
            hs = slice(h * 512, (h + 1) * 512)
            if v % 2 == 0:
                nc.vector.scalar_tensor_tensor(
                    out=junk[:], in0=e32[NP + v][:, hs], scalar=1.0, in1=bc[h][:],
                    op0=ALU.mult, op1=ALU.mult, accum_out=svh[:, v, h:h + 1])
            else:
                i = v // 2 % 2
                pr = big.tile([P, 512], F32, name="prod%d" % i, offset=OFF_GRP + i * 2 * KB)
                nc.vector.tensor_tensor(out=pr[:], in0=e32[NP + v][:, hs], in1=bc[h][:], op=ALU.mult)
                nc.scalar.activation(out=sjunk[:], in_=pr[:], func=ACT.Copy,
                                     accum_out=svh[:, v, h:h + 1])

        def b_steps(h, last):
            js = slice(4 * h, 4 * h + 4)
            sums = [
                lambda: nc.vector.tensor_reduce(out=tt[:, js], in_=csp_of[h][:, :, :, :],
                                                axis=AX.XY, op=ALU.add),
                lambda: nc.vector.tensor_tensor(out=tt[:, js], in0=tt[:, js], in1=acs[:, js], op=ALU.add),
            ]
            if last:
                return sums + [lambda: nc.vector.reciprocal(out=bv[:, js], in_=tt[:, js])]
            return sums + [
                lambda: inverse_and_high(bv[:, js], mvb[:, js, :], tt[:, js], False),
                lambda: low_half(bv[:, js], mvb[:, js, :]),
            ]

        def p_steps(g):
            cs = slice(P_PARTS[g][0], P_PARTS[g][1])
            return [
                lambda: nc.vector.tensor_reduce(out=s_all[:, cs], in_=rsp[g][:],
                                                axis=AX.XY, op=ALU.add),
                lambda: inverse_and_high(a_all[:, cs], mva[:, cs, :], s_all[:, cs], False),
                lambda: low_half(a_all[:, cs], mva[:, cs, :]),
            ]

        def v_steps(lo, hi):
            cs = slice(NP + lo, NP + hi)
            return [
                lambda: nc.vector.tensor_reduce(out=s_all[:, cs], in_=svh[:, lo:hi, :],
                                                axis=AX.X, op=ALU.add),
                lambda: nc.vector.reciprocal(out=a_all[:, cs], in_=s_all[:, cs]),
            ]

        r32 = {}

        def scale_rows(c):
            nc.scalar.activation(out=r32[c][:], in_=r32[c][:], func=ACT.Copy, scale=a_all[:, c:c + 1])

        for jc in range(CC):
            col_pe(jc, 2, FIRST_PARTS)
        for i in range(2):
            acc_turn(i)
            for part in range(2):
                do_eb_transposes(NP - 2 + i, part, 2 + 2 * i + part)
        for f in b_steps(0, False):
            f()
        for i in range(2):
            do_eb_copy(NP - 2 + i, 0, False)
            do_eb_copy(NP - 2 + i, 1, True)

        for it in range(1, ITERS):
            last = it == ITERS - 1
            broadcast(0)
            for g in range(2):
                rsp[g] = bank(4 + g, [P, P_PARTS[g][1] - P_PARTS[g][0], 2, NCOL], F32, "rsp")
            rows_pe(0, 0, 12)
            b1 = dict(zip((1, 2, 3, 5), b_steps(1, False)))
            for v in range(NV):
                row_v(v, 0)
                if v in b1:
                    b1[v]()
            broadcast(1)
            rows_pe(0, 12, NP)
            rows_pe(1, 0, NP)
            p0 = p_steps(0)
            v0 = v_steps(0, 7)
            for v in range(NV):
                row_v(v, 1)
                if v == NV - 2:
                    p0[0]()
            for step in (v0[0], p0[1], v0[1], p0[2]):
                step()
            if last:
                for c in range(NP):
                    r32[c] = big.tile([P, COLS], F32, name="r32_%d" % c, offset=OFF_EB + c * 4 * KB)
                    if c < NP - REBUILT:
                        nc.sync.dma_start(out=r32[c][:], in_=ov[:, P_TILES[c], :])
            extra = dict(zip((1, 2, 3, 4, 5), v_steps(7, NV) + p_steps(1)))
            for v in range(NV - 1):
                acc_step(v, 0)
                acc_step(v, 1)
                if v in extra:
                    extra[v]()
            for h in range(2):
                csp_of[h] = bank(h, [P, 4, 2, NCOL], F32, "csp")
            cols_pe(0, 0, CC)
            if last:
                for c in range(3):
                    scale_rows(c)
            cols_pe(1, 0, 6)
            b0 = b_steps(0, last)
            b0[0]()
            acc_step(NV - 1, 0)
            acc_step(NV - 1, 1)
            acc_turn(0)
            acc_turn(1)
            cols_pe(1, 6, CC)
            for f in b0[1:]:
                f()

        def out_v(v, h):
            hs = slice(h * 512, (h + 1) * 512)
            nc.vector.scalar_tensor_tensor(
                out=e32[NP + v][:, hs], in0=e32[NP + v][:, hs], scalar=a_all[:, NP + v:NP + v + 1],
                in1=bc[h][:], op0=ALU.mult, op1=ALU.mult)

        def out_g(c, cols):
            nc.gpsimd.tensor_tensor(out=r32[c][:, cols], in0=r32[c][:, cols], in1=bcs[:, cols],
                                    op=ALU.mult)

        broadcast(0)
        spread(0)
        b1 = b_steps(1, True)
        for v in range(4):
            out_v(v, 0)
            nc.sync.dma_start(out=ov[:, V_TILES[v], 0:512], in_=e32[NP + v][:, 0:512])
            if v < 3:
                b1[v]()
        for c in range(2):
            out_g(c, slice(0, 512))
        broadcast(1)
        spread(1)
        sum_banks = [(4, 5), (6, 7), (0, 1)]
        esum = {}

        def rebuild(i):
            c = NP - REBUILT + i
            for h in range(2):
                hs = slice(h * 512, (h + 1) * 512)
                e = bank(sum_banks[i % 3][h], [P, 512], F32, "esum")
                nc.tensor.matmul(e[:], lhsT=ident_b[:], rhs=ehi[c][:, hs], start=True, stop=False)
                nc.tensor.matmul(e[:], lhsT=ident_b[:], rhs=elo[c][:, hs], start=False, stop=True)
                esum[(c, h)] = e

        for i in range(3):
            rebuild(i)
        for c in range(3, NP - REBUILT):
            scale_rows(c)
        for c in range(NP - REBUILT):
            out_g(c, slice(512, COLS) if c < 2 else slice(0, COLS))
            nc.scalar.dma_start(out=ov[:, P_TILES[c], :], in_=r32[c][:])
        for v in range(NV):
            cols = slice(512, COLS) if v < 4 else slice(0, COLS)
            if v >= 4:
                out_v(v, 0)
            out_v(v, 1)
            nc.sync.dma_start(out=ov[:, V_TILES[v], cols], in_=e32[NP + v][:, cols])
        for i in range(REBUILT):
            c = NP - REBUILT + i
            for h in range(2):
                hs = slice(h * 512, (h + 1) * 512)
                nc.vector.scalar_tensor_tensor(
                    out=r32[c][:, hs], in0=esum[(c, h)][:], scalar=a_all[:, c:c + 1],
                    in1=bcs[:, hs], op0=ALU.mult, op1=ALU.mult)
            if i + 3 < REBUILT:
                rebuild(i + 3)
            nc.sync.dma_start(out=ov[:, P_TILES[c], :], in_=r32[c][:])
